import numpy as np
import ml_dtypes


def mxq(x, axis, fmt="e4m3"):
    dtype, down = {"e4m3": (ml_dtypes.float8_e4m3fn, 7), "e5m2": (ml_dtypes.float8_e5m2, 14)}[fmt]
    v = np.moveaxis(np.asarray(x, np.float32).astype(ml_dtypes.bfloat16).astype(np.float64), axis, -1)
    blocks = v.reshape(v.shape[:-1] + (-1, 32))
    amax = np.abs(blocks).max(-1, keepdims=True)
    byte = np.maximum(np.where(amax > 0, np.frexp(amax)[1] - 1 + 127, 0) - down, 1)
    scale = np.exp2(byte - 127.0)
    codes = (blocks / scale).astype(np.float32).astype(dtype).astype(np.float64)
    return np.moveaxis((codes * scale).reshape(v.shape), -1, axis)


WIDE = False


def mx_kscale(k):
    if not WIDE:
        return np.ones(k)
    levels = np.array([10, -10, 5, -5, 0])
    a = np.random.permutation(np.resize(levels, k // 512 * 4)).reshape(k // 512, 4)
    idx = np.arange(k)
    return np.exp2(a[idx // 512, idx % 128 // 32])


BF16 = ml_dtypes.bfloat16


def bf(x):
    return np.asarray(x, np.float32).astype(BF16)


def f64(x):
    return np.asarray(x).astype(np.float64)


B, DETER, STOCH, ACT, HID, BLOCKS, NIN, NG = 64, 1024, 1024, 512, 512, 2, 3, 3
DPB = DETER // BLOCKS
EPS = 1e-4


def silu(v):
    return v / (1.0 + np.exp(-v))


def sigmoid(v):
    return 1.0 / (1.0 + np.exp(-v))


def rmsnorm(v, g):
    return v * (1.0 / np.sqrt(np.mean(v * v, axis=-1, keepdims=True) + EPS)) * g


def setup_inputs():
    s = mx_kscale(DETER)
    n = np.random.standard_normal
    return {"hid0": bf(silu(n((B, DETER))) * s), "deter": bf(n((B, DETER))),
            "hw1": bf(n((BLOCKS, DPB, DPB)) * 1.5 / np.sqrt(DPB) / s.reshape(BLOCKS, DPB, 1)), "hb1": bf(n(DETER) * 0.1), "hg1": bf(1.0 + n(DETER) * 0.1),
            "gw": bf(n((BLOCKS, DPB, NG * DPB)) * 2.0 / np.sqrt(DPB)), "gb": bf(n(NG * DETER) * 0.2)}


def block_linear(vq, wq, b):
    y = vq.transpose(1, 0, 2) @ wq
    return y.transpose(1, 0, 2).reshape(B, -1) + b


def reference(hid0, deter, hw1, hb1, hg1, gw, gb):
    u = block_linear(mxq(f64(hid0).reshape(B, BLOCKS, DPB), 2, "e4m3"), mxq(f64(hw1), 1, "e4m3"), f64(hb1))
    h = silu(rmsnorm(u, f64(hg1)))
    p = block_linear(mxq(h.reshape(B, BLOCKS, DPB), 2, "e4m3"), mxq(f64(gw), 1, "e4m3"), f64(gb))
    g = p.reshape(B, BLOCKS, NG, DPB)
    reset = sigmoid(g[:, :, 0, :].reshape(B, DETER))
    cand = np.tanh(reset * g[:, :, 1, :].reshape(B, DETER))
    update = sigmoid(g[:, :, 2, :].reshape(B, DETER) - 1.0)
    return update * cand + (1.0 - update) * f64(deter)

@@ -1,0 +1,314 @@
+import concourse.mybir as mybir
+from concourse.masks import make_identity
+
+F32 = mybir.dt.float32
+BF16 = mybir.dt.bfloat16
+U32 = mybir.dt.uint32
+U8 = mybir.dt.uint8
+FP8X4 = mybir.dt.float8_e4m3fn_x4
+ACT = mybir.ActivationFunctionType
+ALU = mybir.AluOpType
+
+P = 128
+PACK = 4
+B = 64
+BLOCKS = 2
+DPB = 512
+GATES = 3
+R_GATE, C_GATE, Z_GATE = 0, 1, 2
+CHUNKS = DPB // P
+PAIRS = CHUNKS // 2
+EPS = 1e-4
+L1_VECTOR_COLS = 352
+L2_VECTOR_COLS = 256
+
+FLOPS = 2 * B * BLOCKS * (DPB * DPB + DPB * GATES * DPB)
+
+HB_COL = 0
+HG_COL = BLOCKS * CHUNKS
+GB_COL = 2 * BLOCKS * CHUNKS
+VEC_COLS = GB_COL + BLOCKS * GATES * CHUNKS
+
+
+def tile_deter_pb_s_kernel(tc, hid0, deter, hw1, hb1, hg1, gw, gb, out):
+    nc = tc.nc
+    with tc.tile_pool(name="keep", bufs=1) as keep, tc.psum_pool(name="psum", bufs=1) as psum, tc.manual_schedule():
+        layer1_keys = [("w1", j) for j in range(BLOCKS)]
+        layer2_keys = [(g, j) for j in range(BLOCKS) for g in range(GATES)]
+        raw, grouped, codes, scales = {}, {}, {}, {}
+        for key in layer1_keys + layer2_keys:
+            label = "%s_%d" % key
+            raw[key] = keep.tile([P, PACK, DPB], BF16, name="raw_" + label)
+            grouped[key] = keep.tile([P, DPB, PACK], BF16, name="grouped_" + label, align_bytes=64)
+            codes[key] = keep.tile([P, DPB], U32, name="codes_" + label, align_bytes=64)
+            scales[key] = keep.tile([P, DPB], U8, name="scales_" + label, align_bytes=64)
+
+        def load_weights(key):
+            if key[0] == "w1":
+                rows = hw1[key[1]].rearrange("(p t) n -> p t n", t=PACK)
+            else:
+                g, j = key
+                rows = gw[j, :, g * DPB : (g + 1) * DPB].rearrange("(t p) n -> p t n", p=P)
+            nc.sync.dma_start(out=raw[key][:], in_=rows)
+
+        def regroup_on_vector(key, vector_cols):
+            nc.vector.tensor_copy(
+                out=grouped[key][:, 0:vector_cols, :].rearrange("p (c i) t -> p c t i", i=4),
+                in_=raw[key][:, :, 0:vector_cols].rearrange("p t (c i) -> p c t i", i=4),
+            )
+
+        def regroup_on_scalar(key, vector_cols):
+            nc.scalar.copy(
+                out=grouped[key][:, vector_cols:DPB, :].rearrange("p (c i) t -> p c t i", i=4),
+                in_=raw[key][:, :, vector_cols:DPB].rearrange("p t (c i) -> p c t i", i=4),
+            )
+
+        def regroup(key, vector_cols):
+            regroup_on_vector(key, vector_cols)
+            regroup_on_scalar(key, vector_cols)
+
+        def quantise(key):
+            nc.vector.quantize_mx(
+                out=codes[key][:].bitcast(FP8X4),
+                scales=scales[key][:],
+                in_=grouped[key][:].rearrange("p w t -> p (w t)"),
+            )
+
+        def multiply(key, acc, moving_codes, moving_scales):
+            j = key[1]
+            for m in range(CHUNKS):
+                nc.tensor.matmul_mx(
+                    out=acc[:, m, :],
+                    lhsT=codes[key][:, m * P : (m + 1) * P].bitcast(FP8X4),
+                    lhsT_scale=scales[key][:, m * P : (m + 1) * P],
+                    rhs=moving_codes[:, j * B : (j + 1) * B].bitcast(FP8X4),
+                    rhs_scale=moving_scales[:, j * B : (j + 1) * B],
+                    start=True,
+                    stop=True,
+                )
+
+        ident_f32 = keep.tile([P, P], F32, name="ident_f32")
+        make_identity(nc, ident_f32[:])
+        ident_bf = keep.tile([P, P], BF16, name="ident_bf")
+        make_identity(nc, ident_bf[:])
+        mean_w = keep.tile([P, P], F32, name="mean_w")
+        nc.vector.memset(mean_w[:], 1.0 / (BLOCKS * DPB))
+        eps_col = keep.tile([P, 1], F32, name="eps_col")
+        nc.vector.memset(eps_col[:], EPS)
+        one_col = keep.tile([P, 1], F32, name="one_col")
+        nc.vector.memset(one_col[:], 1.0)
+        warm_col = keep.tile([P, 2], F32, name="warm_col")
+        nc.scalar.activation(out=warm_col[:, 0:1], in_=one_col[:], func=ACT.Sqrt)
+
+        x_sb = keep.tile([P, DPB], BF16, name="x_sb")
+        vec_rows = keep.tile([P, P], BF16, name="vec_rows")
+        d_tok = keep.tile([P, BLOCKS * PAIRS, P], BF16, name="d_tok")
+        nc.vector.memset(vec_rows[:], 0.0)
+        deter_view = deter.rearrange("b (q h f) -> h b q f", h=2, f=P)
+        out_view = out.rearrange("b (q h f) -> h b q f", h=2, f=P)
+
+        load_weights(("w1", 0))
+        for j in range(BLOCKS):
+            nc.sync.dma_start(out=x_sb[j * B : (j + 1) * B, :], in_=hid0[:, j * DPB : (j + 1) * DPB])
+        load_weights(("w1", 1))
+        nc.sync.dma_start(out=vec_rows[HB_COL:HG_COL, :], in_=hb1.rearrange("(r p) -> r p", p=P))
+        nc.sync.dma_start(out=vec_rows[HG_COL:GB_COL, :], in_=hg1.rearrange("(r p) -> r p", p=P))
+        nc.sync.dma_start(out=vec_rows[GB_COL:VEC_COLS, :], in_=gb.rearrange("(r p) -> r p", p=P))
+        load_weights((R_GATE, 0))
+        load_weights((C_GATE, 0))
+        for h in range(2):
+            nc.sync.dma_start(out=d_tok[h * B : (h + 1) * B, :, :], in_=deter_view[h])
+        load_weights((Z_GATE, 0))
+        load_weights((R_GATE, 1))
+        load_weights((C_GATE, 1))
+        load_weights((Z_GATE, 1))
+
+        xT_ps = psum.tile([P, 2, P], F32, name="xT_ps", tag="bank_0")
+        vecT_ps = psum.tile([P, P], BF16, name="vecT_ps", tag="bank_1")
+        dT_ps = psum.tile([P, BLOCKS, CHUNKS, B], BF16, name="dT_ps", tag="bank_2")
+        u_ps = [psum.tile([P, CHUNKS, B], F32, name="u_ps_%d" % j, tag="bank_%d" % (3 + j)) for j in range(BLOCKS)]
+
+        x_words = x_sb[:].bitcast(F32).rearrange("p (w u) -> p u w", u=2)
+        for u in range(2):
+            nc.tensor.transpose(xT_ps[:, u, :], x_words[:, u, :], ident_f32[:])
+        x_grouped = keep.tile([P, P * PACK], BF16, name="x_grouped", align_bytes=64)
+        nc.vector.tensor_copy(
+            out=x_grouped[:].bitcast(F32).rearrange("p (c u) -> p c u", u=2),
+            in_=xT_ps[:].rearrange("p u c -> p c u"),
+        )
+        x_codes = keep.tile([P, P], U32, name="x_codes", align_bytes=64)
+        x_scales = keep.tile([P, P], U8, name="x_scales", align_bytes=64)
+
+        regroup(("w1", 0), L1_VECTOR_COLS)
+        nc.vector.quantize_mx(out=x_codes[:].bitcast(FP8X4), scales=x_scales[:], in_=x_grouped[:])
+        quantise(("w1", 0))
+        multiply(("w1", 0), u_ps[0], x_codes, x_scales)
+
+        nc.tensor.transpose(vecT_ps[:], vec_rows[:], ident_bf[:])
+        vec = keep.tile([P, VEC_COLS], F32, name="vec")
+        nc.vector.tensor_copy(out=vec[:], in_=vecT_ps[:, 0:VEC_COLS])
+        z_bias = vec[:, GB_COL:VEC_COLS].rearrange("p (j g m) -> p j g m", j=BLOCKS, g=GATES)[:, :, Z_GATE, :]
+        nc.vector.tensor_scalar(out=z_bias, in0=z_bias, scalar1=-1.0, scalar2=None, op0=ALU.add)
+
+        def vec_col(first, c):
+            return vec[:, first + c : first + c + 1]
+
+        sq = keep.tile([P, BLOCKS, CHUNKS, B], F32, name="sq")
+        gained = keep.tile([P, BLOCKS, CHUNKS, B], F32, name="gained")
+        normed = keep.tile([P, BLOCKS, CHUNKS, B], F32, name="normed")
+        gate_h = keep.tile([P, BLOCKS, CHUNKS, B], F32, name="gate_h")
+        h_grouped = keep.tile([P, BLOCKS, B, PACK], BF16, name="h_grouped", align_bytes=64)
+        mean_ps = psum.tile([P, B], F32, name="mean_ps", tag="bank_0")
+        std = keep.tile([P, B], F32, name="std")
+        rstd = keep.tile([P, B], F32, name="rstd")
+
+        def squares(j):
+            for m in range(CHUNKS):
+                c = j * CHUNKS + m
+                nc.scalar.activation(
+                    out=sq[:, j, m, :], in_=u_ps[j][:, m, :], func=ACT.Square, bias=vec_col(HB_COL, c), scale=1.0
+                )
+                nc.tensor.matmul(
+                    out=mean_ps[:], lhsT=mean_w[:], rhs=sq[:, j, m, :],
+                    start=(c == 0), stop=(c == BLOCKS * CHUNKS - 1),
+                )
+
+        def bias_and_gain(j):
+            for m in range(CHUNKS):
+                c = j * CHUNKS + m
+                nc.vector.tensor_scalar(
+                    out=gained[:, j, m, :], in0=u_ps[j][:, m, :],
+                    scalar1=vec_col(HB_COL, c), scalar2=vec_col(HG_COL, c), op0=ALU.add, op1=ALU.mult,
+                )
+
+        def normalise(j):
+            nc.vector.tensor_tensor(
+                out=normed[:, j], in0=gained[:, j], in1=rstd[:].unsqueeze(1).to_broadcast([P, CHUNKS, B]), op=ALU.mult
+            )
+
+        def silu_gate(j):
+            nc.scalar.activation(
+                out=gate_h[:, j].rearrange("p t b -> p (t b)"), in_=normed[:, j].rearrange("p t b -> p (t b)"),
+                func=ACT.Sigmoid,
+            )
+
+        def silu_product(j):
+            nc.vector.tensor_tensor(
+                out=h_grouped[:, j], in0=normed[:, j].rearrange("p t b -> p b t"),
+                in1=gate_h[:, j].rearrange("p t b -> p b t"), op=ALU.mult,
+            )
+
+        regroup(("w1", 1), L1_VECTOR_COLS)
+        regroup((R_GATE, 0), L2_VECTOR_COLS)
+        quantise(("w1", 1))
+        multiply(("w1", 1), u_ps[1], x_codes, x_scales)
+        squares(0)
+        regroup((C_GATE, 0), L2_VECTOR_COLS)
+        bias_and_gain(0)
+        squares(1)
+        for q in range(BLOCKS * PAIRS):
+            nc.tensor.transpose(
+                dT_ps[:].rearrange("p j m b -> p (j m b)")[:, q * P : (q + 1) * P], d_tok[:, q, :], ident_bf[:]
+            )
+        regroup((Z_GATE, 0), L2_VECTOR_COLS)
+        quantise((R_GATE, 0))
+        bias_and_gain(1)
+        quantise((C_GATE, 0))
+        nc.scalar.activation(out=std[:], in_=mean_ps[:], func=ACT.Sqrt, bias=eps_col[:], scale=1.0)
+        nc.scalar.activation(out=warm_col[:, 1:2], in_=one_col[:], func=ACT.Sigmoid)
+        regroup_on_vector((R_GATE, 1), L2_VECTOR_COLS)
+        nc.vector.reciprocal(out=rstd[:], in_=std[:])
+        normalise(0)
+        normalise(1)
+        silu_gate(0)
+        silu_gate(1)
+        regroup_on_scalar((R_GATE, 1), L2_VECTOR_COLS)
+        regroup((C_GATE, 1), L2_VECTOR_COLS)
+        quantise((Z_GATE, 0))
+        silu_product(0)
+        silu_product(1)
+        h_codes = keep.tile([P, P], U32, name="h_codes", align_bytes=64)
+        h_scales = keep.tile([P, P], U8, name="h_scales", align_bytes=64)
+        nc.vector.quantize_mx(
+            out=h_codes[:].bitcast(FP8X4), scales=h_scales[:], in_=h_grouped[:].rearrange("p j b t -> p (j b t)")
+        )
+        quantise((R_GATE, 1))
+        regroup((Z_GATE, 1), L2_VECTOR_COLS)
+        quantise((C_GATE, 1))
+        quantise((Z_GATE, 1))
+
+        gate_ps = {}
+        for j in range(BLOCKS):
+            gate_ps[(R_GATE, j)] = psum.tile([P, CHUNKS, B], F32, name="r_ps_%d" % j, tag="bank_%d" % (3 + j))
+        gate_ps[(C_GATE, 0)] = psum.tile([P, CHUNKS, B], F32, name="c_ps_0", tag="bank_1")
+        gate_ps[(C_GATE, 1)] = psum.tile([P, CHUNKS, B], F32, name="c_ps_1", tag="bank_5")
+        gate_ps[(Z_GATE, 0)] = psum.tile([P, CHUNKS, B], F32, name="z_ps_0", tag="bank_6")
+        gate_ps[(Z_GATE, 1)] = psum.tile([P, CHUNKS, B], F32, name="z_ps_1", tag="bank_7")
+
+        reset = keep.tile([P, BLOCKS, CHUNKS, B], F32, name="reset")
+        rc = keep.tile([P, BLOCKS, CHUNKS, B], F32, name="rc")
+        cand = keep.tile([P, BLOCKS, CHUNKS, B], F32, name="cand")
+        diff = keep.tile([P, BLOCKS, CHUNKS, B], F32, name="diff")
+        update = keep.tile([P, BLOCKS, CHUNKS, B], F32, name="update")
+        step = keep.tile([P, BLOCKS, CHUNKS, B], F32, name="step")
+        result = keep.tile([P, BLOCKS, PAIRS, P], F32, name="result")
+
+        def sigmoid_gate(g, j, dest):
+            for m in range(CHUNKS):
+                nc.scalar.activation(
+                    out=dest[:, j, m, :], in_=gate_ps[(g, j)][:, m, :], func=ACT.Sigmoid,
+                    bias=vec_col(GB_COL, (j * GATES + g) * CHUNKS + m), scale=1.0,
+                )
+
+        def reset_candidate(j):
+            for m in range(CHUNKS):
+                nc.vector.scalar_tensor_tensor(
+                    out=rc[:, j, m, :], in0=gate_ps[(C_GATE, j)][:, m, :],
+                    scalar=vec_col(GB_COL, (j * GATES + C_GATE) * CHUNKS + m),
+                    in1=reset[:, j, m, :], op0=ALU.add, op1=ALU.mult,
+                )
+
+        def candidate(j):
+            nc.scalar.activation(
+                out=cand[:, j].rearrange("p m b -> p (m b)"), in_=rc[:, j].rearrange("p m b -> p (m b)"), func=ACT.Tanh
+            )
+
+        def difference(j):
+            nc.vector.tensor_tensor(out=diff[:, j], in0=cand[:, j], in1=dT_ps[:, j], op=ALU.subtract)
+
+        def weighted_step(j):
+            nc.vector.tensor_tensor(out=step[:, j], in0=update[:, j], in1=diff[:, j], op=ALU.mult)
+
+        def finish(j):
+            stepT_ps = psum.tile([P, PAIRS, P], F32, name="stepT_ps_%d" % j, tag="bank_%d" % (3 + j))
+            for q in range(PAIRS):
+                nc.tensor.transpose(
+                    stepT_ps[:, q, :], step[:, j, 2 * q : 2 * q + 2, :].rearrange("p m b -> p (m b)"), ident_f32[:]
+                )
+            nc.vector.tensor_tensor(
+                out=result[:, j], in0=stepT_ps[:], in1=d_tok[:, j * PAIRS : (j + 1) * PAIRS, :], op=ALU.add
+            )
+            for h in range(2):
+                nc.sync.dma_start(
+                    out=out_view[h][:, j * PAIRS : (j + 1) * PAIRS, :], in_=result[h * B : (h + 1) * B, j, :, :]
+                )
+
+        for j in range(BLOCKS):
+            multiply((R_GATE, j), gate_ps[(R_GATE, j)], h_codes, h_scales)
+        for j in range(BLOCKS):
+            multiply((C_GATE, j), gate_ps[(C_GATE, j)], h_codes, h_scales)
+            multiply((Z_GATE, j), gate_ps[(Z_GATE, j)], h_codes, h_scales)
+        sigmoid_gate(R_GATE, 0, reset)
+        sigmoid_gate(R_GATE, 1, reset)
+        reset_candidate(0)
+        sigmoid_gate(Z_GATE, 0, update)
+        reset_candidate(1)
+        candidate(0)
+        candidate(1)
+        sigmoid_gate(Z_GATE, 1, update)
+        difference(0)
+        weighted_step(0)
+        difference(1)
+        weighted_step(1)
+        finish(0)
+        finish(1)

@@ -19,8 +19,13 @@ R_GATE, C_GATE, Z_GATE = 0, 1, 2
 CHUNKS = DPB // P
 PAIRS = CHUNKS // 2
 EPS = 1e-4
-L1_VECTOR_COLS = 352
-L2_VECTOR_COLS = 256
+
+WHOLE = (0, DPB)
+FIRST_HALF = (0, DPB // 2)
+SECOND_HALF = (DPB // 2, DPB)
+
+L1_VECTOR_SHARE = 11
+L2_VECTOR_SHARE = 8
 
 FLOPS = 2 * B * BLOCKS * (DPB * DPB + DPB * GATES * DPB)
 
@@ -43,40 +48,49 @@ def tile_deter_pb_s_kernel(tc, hid0, deter, hw1, hb1, hg1, gw, gb, out):
             codes[key] = keep.tile([P, DPB], U32, name="codes_" + label, align_bytes=64)
             scales[key] = keep.tile([P, DPB], U8, name="scales_" + label, align_bytes=64)
 
-        def load_weights(key):
+        def load_weights(key, cols):
+            lo, hi = cols
             if key[0] == "w1":
-                rows = hw1[key[1]].rearrange("(p t) n -> p t n", t=PACK)
+                rows = hw1[key[1], :, lo:hi].rearrange("(p t) n -> p t n", t=PACK)
             else:
                 g, j = key
-                rows = gw[j, :, g * DPB : (g + 1) * DPB].rearrange("(t p) n -> p t n", p=P)
-            nc.sync.dma_start(out=raw[key][:], in_=rows)
+                rows = gw[j, :, g * DPB + lo : g * DPB + hi].rearrange("(t p) n -> p t n", p=P)
+            nc.sync.dma_start(out=raw[key][:, :, lo:hi], in_=rows)
 
-        def regroup_on_vector(key, vector_cols):
+        def split(key, cols):
+            lo, hi = cols
+            share = L1_VECTOR_SHARE if key[0] == "w1" else L2_VECTOR_SHARE
+            return lo, lo + (hi - lo) * share // 16, hi
+
+        def regroup_on_vector(key, cols):
+            lo, mid, hi = split(key, cols)
             nc.vector.tensor_copy(
-                out=grouped[key][:, 0:vector_cols, :].rearrange("p (c i) t -> p c t i", i=4),
-                in_=raw[key][:, :, 0:vector_cols].rearrange("p t (c i) -> p c t i", i=4),
+                out=grouped[key][:, lo:mid, :].rearrange("p (c i) t -> p c t i", i=4),
+                in_=raw[key][:, :, lo:mid].rearrange("p t (c i) -> p c t i", i=4),
             )
 
-        def regroup_on_scalar(key, vector_cols):
+        def regroup_on_scalar(key, cols):
+            lo, mid, hi = split(key, cols)
             nc.scalar.copy(
-                out=grouped[key][:, vector_cols:DPB, :].rearrange("p (c i) t -> p c t i", i=4),
-                in_=raw[key][:, :, vector_cols:DPB].rearrange("p t (c i) -> p c t i", i=4),
+                out=grouped[key][:, mid:hi, :].rearrange("p (c i) t -> p c t i", i=4),
+                in_=raw[key][:, :, mid:hi].rearrange("p t (c i) -> p c t i", i=4),
             )
 
-        def regroup(key, vector_cols):
-            regroup_on_vector(key, vector_cols)
-            regroup_on_scalar(key, vector_cols)
+        def regroup(key, cols):
+            regroup_on_vector(key, cols)
+            regroup_on_scalar(key, cols)
 
-        def quantise(key):
+        def quantise(key, cols):
+            lo, hi = cols
             nc.vector.quantize_mx(
-                out=codes[key][:].bitcast(FP8X4),
-                scales=scales[key][:],
-                in_=grouped[key][:].rearrange("p w t -> p (w t)"),
+                out=codes[key][:, lo:hi].bitcast(FP8X4),
+                scales=scales[key][:, lo:hi],
+                in_=grouped[key][:, lo:hi, :].rearrange("p w t -> p (w t)"),
             )
 
-        def multiply(key, acc, moving_codes, moving_scales):
+        def multiply(key, cols, acc, moving_codes, moving_scales):
             j = key[1]
-            for m in range(CHUNKS):
+            for m in range(cols[0] // P, cols[1] // P):
                 nc.tensor.matmul_mx(
                     out=acc[:, m, :],
                     lhsT=codes[key][:, m * P : (m + 1) * P].bitcast(FP8X4),
@@ -91,42 +105,47 @@ def tile_deter_pb_s_kernel(tc, hid0, deter, hw1, hb1, hg1, gw, gb, out):
         make_identity(nc, ident_f32[:])
         ident_bf = keep.tile([P, P], BF16, name="ident_bf")
         make_identity(nc, ident_bf[:])
+        vec_rows = keep.tile([P, P], BF16, name="vec_rows")
+        nc.vector.memset(vec_rows[:], 0.0)
+        one_col = keep.tile([P, 1], F32, name="one_col")
+        nc.vector.memset(one_col[:], 1.0)
+        warm_col = keep.tile([P, 2], F32, name="warm_col")
+        nc.scalar.activation(out=warm_col[:, 0:1], in_=one_col[:], func=ACT.Abs_reciprocal_sqrt)
         mean_w = keep.tile([P, P], F32, name="mean_w")
         nc.vector.memset(mean_w[:], 1.0 / (BLOCKS * DPB))
         eps_col = keep.tile([P, 1], F32, name="eps_col")
         nc.vector.memset(eps_col[:], EPS)
-        one_col = keep.tile([P, 1], F32, name="one_col")
-        nc.vector.memset(one_col[:], 1.0)
-        warm_col = keep.tile([P, 2], F32, name="warm_col")
-        nc.scalar.activation(out=warm_col[:, 0:1], in_=one_col[:], func=ACT.Sqrt)
 
         x_sb = keep.tile([P, DPB], BF16, name="x_sb")
-        vec_rows = keep.tile([P, P], BF16, name="vec_rows")
         d_tok = keep.tile([P, BLOCKS * PAIRS, P], BF16, name="d_tok")
-        nc.vector.memset(vec_rows[:], 0.0)
         deter_view = deter.rearrange("b (q h f) -> h b q f", h=2, f=P)
         out_view = out.rearrange("b (q h f) -> h b q f", h=2, f=P)
-
-        load_weights(("w1", 0))
         for j in range(BLOCKS):
             nc.sync.dma_start(out=x_sb[j * B : (j + 1) * B, :], in_=hid0[:, j * DPB : (j + 1) * DPB])
-        load_weights(("w1", 1))
+        load_weights(("w1", 0), FIRST_HALF)
+        load_weights(("w1", 0), SECOND_HALF)
         nc.sync.dma_start(out=vec_rows[HB_COL:HG_COL, :], in_=hb1.rearrange("(r p) -> r p", p=P))
         nc.sync.dma_start(out=vec_rows[HG_COL:GB_COL, :], in_=hg1.rearrange("(r p) -> r p", p=P))
         nc.sync.dma_start(out=vec_rows[GB_COL:VEC_COLS, :], in_=gb.rearrange("(r p) -> r p", p=P))
-        load_weights((R_GATE, 0))
-        load_weights((C_GATE, 0))
+        load_weights(("w1", 1), WHOLE)
+        for g in range(GATES):
+            load_weights((g, 0), WHOLE)
         for h in range(2):
             nc.sync.dma_start(out=d_tok[h * B : (h + 1) * B, :, :], in_=deter_view[h])
-        load_weights((Z_GATE, 0))
-        load_weights((R_GATE, 1))
-        load_weights((C_GATE, 1))
-        load_weights((Z_GATE, 1))
+        load_weights((R_GATE, 1), WHOLE)
+        load_weights((C_GATE, 1), WHOLE)
+        load_weights((Z_GATE, 1), FIRST_HALF)
+        load_weights((Z_GATE, 1), SECOND_HALF)
 
         xT_ps = psum.tile([P, 2, P], F32, name="xT_ps", tag="bank_0")
         vecT_ps = psum.tile([P, P], BF16, name="vecT_ps", tag="bank_1")
         dT_ps = psum.tile([P, BLOCKS, CHUNKS, B], BF16, name="dT_ps", tag="bank_2")
         u_ps = [psum.tile([P, CHUNKS, B], F32, name="u_ps_%d" % j, tag="bank_%d" % (3 + j)) for j in range(BLOCKS)]
+
+        regroup(("w1", 0), FIRST_HALF)
+        regroup(("w1", 0), SECOND_HALF)
+        quantise(("w1", 0), FIRST_HALF)
+        quantise(("w1", 0), SECOND_HALF)
 
         x_words = x_sb[:].bitcast(F32).rearrange("p (w u) -> p u w", u=2)
         for u in range(2):
@@ -139,39 +158,41 @@ def tile_deter_pb_s_kernel(tc, hid0, deter, hw1, hb1, hg1, gw, gb, out):
         x_codes = keep.tile([P, P], U32, name="x_codes", align_bytes=64)
         x_scales = keep.tile([P, P], U8, name="x_scales", align_bytes=64)
 
-        regroup(("w1", 0), L1_VECTOR_COLS)
-        nc.vector.quantize_mx(out=x_codes[:].bitcast(FP8X4), scales=x_scales[:], in_=x_grouped[:])
-        quantise(("w1", 0))
-        multiply(("w1", 0), u_ps[0], x_codes, x_scales)
-
         nc.tensor.transpose(vecT_ps[:], vec_rows[:], ident_bf[:])
         vec = keep.tile([P, VEC_COLS], F32, name="vec")
         nc.vector.tensor_copy(out=vec[:], in_=vecT_ps[:, 0:VEC_COLS])
         z_bias = vec[:, GB_COL:VEC_COLS].rearrange("p (j g m) -> p j g m", j=BLOCKS, g=GATES)[:, :, Z_GATE, :]
         nc.vector.tensor_scalar(out=z_bias, in0=z_bias, scalar1=-1.0, scalar2=None, op0=ALU.add)
+        nc.vector.quantize_mx(out=x_codes[:].bitcast(FP8X4), scales=x_scales[:], in_=x_grouped[:])
 
         def vec_col(first, c):
             return vec[:, first + c : first + c + 1]
 
         sq = keep.tile([P, BLOCKS, CHUNKS, B], F32, name="sq")
+        sq_sum = keep.tile([P, BLOCKS, B], F32, name="sq_sum")
         gained = keep.tile([P, BLOCKS, CHUNKS, B], F32, name="gained")
         normed = keep.tile([P, BLOCKS, CHUNKS, B], F32, name="normed")
         gate_h = keep.tile([P, BLOCKS, CHUNKS, B], F32, name="gate_h")
         h_grouped = keep.tile([P, BLOCKS, B, PACK], BF16, name="h_grouped", align_bytes=64)
+        h_codes = keep.tile([P, P], U32, name="h_codes", align_bytes=64)
+        h_scales = keep.tile([P, P], U8, name="h_scales", align_bytes=64)
         mean_ps = psum.tile([P, B], F32, name="mean_ps", tag="bank_0")
-        std = keep.tile([P, B], F32, name="std")
         rstd = keep.tile([P, B], F32, name="rstd")
 
         def squares(j):
             for m in range(CHUNKS):
-                c = j * CHUNKS + m
                 nc.scalar.activation(
-                    out=sq[:, j, m, :], in_=u_ps[j][:, m, :], func=ACT.Square, bias=vec_col(HB_COL, c), scale=1.0
+                    out=sq[:, j, m, :], in_=u_ps[j][:, m, :], func=ACT.Square,
+                    bias=vec_col(HB_COL, j * CHUNKS + m), scale=1.0,
                 )
-                nc.tensor.matmul(
-                    out=mean_ps[:], lhsT=mean_w[:], rhs=sq[:, j, m, :],
-                    start=(c == 0), stop=(c == BLOCKS * CHUNKS - 1),
-                )
+
+        def mean_of_squares(j):
+            nc.vector.tensor_reduce(
+                out=sq_sum[:, j, :], in_=sq[:, j].rearrange("p m b -> p b m"), op=ALU.add, axis=mybir.AxisListType.X
+            )
+            nc.tensor.matmul(
+                out=mean_ps[:], lhsT=mean_w[:], rhs=sq_sum[:, j, :], start=(j == 0), stop=(j == BLOCKS - 1)
+            )
 
         def bias_and_gain(j):
             for m in range(CHUNKS):
@@ -198,44 +219,36 @@ def tile_deter_pb_s_kernel(tc, hid0, deter, hw1, hb1, hg1, gw, gb, out):
                 in1=gate_h[:, j].rearrange("p t b -> p b t"), op=ALU.mult,
             )
 
-        regroup(("w1", 1), L1_VECTOR_COLS)
-        regroup((R_GATE, 0), L2_VECTOR_COLS)
-        quantise(("w1", 1))
-        multiply(("w1", 1), u_ps[1], x_codes, x_scales)
+        multiply(("w1", 0), WHOLE, u_ps[0], x_codes, x_scales)
+        regroup(("w1", 1), WHOLE)
+        quantise(("w1", 1), WHOLE)
+        multiply(("w1", 1), WHOLE, u_ps[1], x_codes, x_scales)
+        regroup((R_GATE, 0), WHOLE)
         squares(0)
-        regroup((C_GATE, 0), L2_VECTOR_COLS)
-        bias_and_gain(0)
         squares(1)
+        regroup((C_GATE, 0), WHOLE)
+        quantise((R_GATE, 0), WHOLE)
+        mean_of_squares(0)
+        regroup((Z_GATE, 0), WHOLE)
+        mean_of_squares(1)
+        quantise((C_GATE, 0), WHOLE)
+        bias_and_gain(0)
+        bias_and_gain(1)
+        nc.scalar.activation(out=rstd[:], in_=mean_ps[:], func=ACT.Abs_reciprocal_sqrt, bias=eps_col[:], scale=1.0)
+        nc.scalar.activation(out=warm_col[:, 1:2], in_=one_col[:], func=ACT.Sigmoid)
+        for j in range(BLOCKS):
+            normalise(j)
+            silu_gate(j)
+        quantise((Z_GATE, 0), WHOLE)
+        for j in range(BLOCKS):
+            silu_product(j)
+        nc.vector.quantize_mx(
+            out=h_codes[:].bitcast(FP8X4), scales=h_scales[:], in_=h_grouped[:].rearrange("p j b t -> p (j b t)")
+        )
         for q in range(BLOCKS * PAIRS):
             nc.tensor.transpose(
                 dT_ps[:].rearrange("p j m b -> p (j m b)")[:, q * P : (q + 1) * P], d_tok[:, q, :], ident_bf[:]
             )
-        regroup((Z_GATE, 0), L2_VECTOR_COLS)
-        quantise((R_GATE, 0))
-        bias_and_gain(1)
-        quantise((C_GATE, 0))
-        nc.scalar.activation(out=std[:], in_=mean_ps[:], func=ACT.Sqrt, bias=eps_col[:], scale=1.0)
-        nc.scalar.activation(out=warm_col[:, 1:2], in_=one_col[:], func=ACT.Sigmoid)
-        regroup_on_vector((R_GATE, 1), L2_VECTOR_COLS)
-        nc.vector.reciprocal(out=rstd[:], in_=std[:])
-        normalise(0)
-        normalise(1)
-        silu_gate(0)
-        silu_gate(1)
-        regroup_on_scalar((R_GATE, 1), L2_VECTOR_COLS)
-        regroup((C_GATE, 1), L2_VECTOR_COLS)
-        quantise((Z_GATE, 0))
-        silu_product(0)
-        silu_product(1)
-        h_codes = keep.tile([P, P], U32, name="h_codes", align_bytes=64)
-        h_scales = keep.tile([P, P], U8, name="h_scales", align_bytes=64)
-        nc.vector.quantize_mx(
-            out=h_codes[:].bitcast(FP8X4), scales=h_scales[:], in_=h_grouped[:].rearrange("p j b t -> p (j b t)")
-        )
-        quantise((R_GATE, 1))
-        regroup((Z_GATE, 1), L2_VECTOR_COLS)
-        quantise((C_GATE, 1))
-        quantise((Z_GATE, 1))
 
         gate_ps = {}
         for j in range(BLOCKS):
@@ -252,11 +265,16 @@ def tile_deter_pb_s_kernel(tc, hid0, deter, hw1, hb1, hg1, gw, gb, out):
         update = keep.tile([P, BLOCKS, CHUNKS, B], F32, name="update")
         step = keep.tile([P, BLOCKS, CHUNKS, B], F32, name="step")
         result = keep.tile([P, BLOCKS, PAIRS, P], F32, name="result")
+        stepT_ps = {}
 
-        def sigmoid_gate(g, j, dest):
-            for m in range(CHUNKS):
+        def gate_product(key, cols):
+            multiply(key, cols, gate_ps[key], h_codes, h_scales)
+
+        def sigmoid_gate(key, cols, dest):
+            g, j = key
+            for m in range(cols[0] // P, cols[1] // P):
                 nc.scalar.activation(
-                    out=dest[:, j, m, :], in_=gate_ps[(g, j)][:, m, :], func=ACT.Sigmoid,
+                    out=dest[:, j, m, :], in_=gate_ps[key][:, m, :], func=ACT.Sigmoid,
                     bias=vec_col(GB_COL, (j * GATES + g) * CHUNKS + m), scale=1.0,
                 )
 
@@ -276,39 +294,62 @@ def tile_deter_pb_s_kernel(tc, hid0, deter, hw1, hb1, hg1, gw, gb, out):
         def difference(j):
             nc.vector.tensor_tensor(out=diff[:, j], in0=cand[:, j], in1=dT_ps[:, j], op=ALU.subtract)
 
-        def weighted_step(j):
-            nc.vector.tensor_tensor(out=step[:, j], in0=update[:, j], in1=diff[:, j], op=ALU.mult)
+        def weighted_step(j, q):
+            pair = slice(2 * q, 2 * q + 2)
+            nc.vector.tensor_tensor(out=step[:, j, pair, :], in0=update[:, j, pair, :], in1=diff[:, j, pair, :], op=ALU.mult)
 
-        def finish(j):
-            stepT_ps = psum.tile([P, PAIRS, P], F32, name="stepT_ps_%d" % j, tag="bank_%d" % (3 + j))
-            for q in range(PAIRS):
-                nc.tensor.transpose(
-                    stepT_ps[:, q, :], step[:, j, 2 * q : 2 * q + 2, :].rearrange("p m b -> p (m b)"), ident_f32[:]
-                )
-            nc.vector.tensor_tensor(
-                out=result[:, j], in0=stepT_ps[:], in1=d_tok[:, j * PAIRS : (j + 1) * PAIRS, :], op=ALU.add
+        def to_tokens(j, q):
+            bank = 3 + j if q == 0 else j
+            stepT_ps[(j, q)] = psum.tile([P, P], F32, name="stepT_ps_%d_%d" % (j, q), tag="bank_%d" % bank)
+            nc.tensor.transpose(
+                stepT_ps[(j, q)][:], step[:, j, 2 * q : 2 * q + 2, :].rearrange("p m b -> p (m b)"), ident_f32[:]
             )
+
+        def add_state(j, q):
+            nc.vector.tensor_tensor(
+                out=result[:, j, q, :], in0=stepT_ps[(j, q)][:], in1=d_tok[:, j * PAIRS + q, :], op=ALU.add
+            )
+
+        def store(j):
             for h in range(2):
                 nc.sync.dma_start(
                     out=out_view[h][:, j * PAIRS : (j + 1) * PAIRS, :], in_=result[h * B : (h + 1) * B, j, :, :]
                 )
 
-        for j in range(BLOCKS):
-            multiply((R_GATE, j), gate_ps[(R_GATE, j)], h_codes, h_scales)
-        for j in range(BLOCKS):
-            multiply((C_GATE, j), gate_ps[(C_GATE, j)], h_codes, h_scales)
-            multiply((Z_GATE, j), gate_ps[(Z_GATE, j)], h_codes, h_scales)
-        sigmoid_gate(R_GATE, 0, reset)
-        sigmoid_gate(R_GATE, 1, reset)
+        regroup((R_GATE, 1), WHOLE)
+        quantise((R_GATE, 1), WHOLE)
+        regroup((C_GATE, 1), WHOLE)
+        quantise((C_GATE, 1), WHOLE)
+        gate_product((R_GATE, 0), WHOLE)
+        gate_product((C_GATE, 0), WHOLE)
+        gate_product((R_GATE, 1), WHOLE)
+        gate_product((Z_GATE, 0), WHOLE)
+        gate_product((C_GATE, 1), WHOLE)
+        regroup((Z_GATE, 1), FIRST_HALF)
+        sigmoid_gate((R_GATE, 0), WHOLE, reset)
         reset_candidate(0)
-        sigmoid_gate(Z_GATE, 0, update)
-        reset_candidate(1)
+        quantise((Z_GATE, 1), FIRST_HALF)
+        regroup((Z_GATE, 1), SECOND_HALF)
+        quantise((Z_GATE, 1), SECOND_HALF)
+        gate_product((Z_GATE, 1), FIRST_HALF)
+        gate_product((Z_GATE, 1), SECOND_HALF)
+
+        sigmoid_gate((R_GATE, 1), WHOLE, reset)
         candidate(0)
-        candidate(1)
-        sigmoid_gate(Z_GATE, 1, update)
         difference(0)
-        weighted_step(0)
+        reset_candidate(1)
+        sigmoid_gate((Z_GATE, 0), WHOLE, update)
+        for q in range(PAIRS):
+            weighted_step(0, q)
+            to_tokens(0, q)
+        candidate(1)
         difference(1)
-        weighted_step(1)
-        finish(0)
-        finish(1)
+        sigmoid_gate((Z_GATE, 1), FIRST_HALF, update)
+        sigmoid_gate((Z_GATE, 1), SECOND_HALF, update)
+        for q in range(PAIRS):
+            weighted_step(1, q)
+            to_tokens(1, q)
+        for j in range(BLOCKS):
+            for q in range(PAIRS):
+                add_state(j, q)
+            store(j)

@@ -151,7 +151,7 @@ def tile_deter_pb_s_kernel(tc, hid0, deter, hw1, hb1, hg1, gw, gb, out):
         for u in range(2):
             nc.tensor.transpose(xT_ps[:, u, :], x_words[:, u, :], ident_f32[:])
         x_grouped = keep.tile([P, P * PACK], BF16, name="x_grouped", align_bytes=64)
-        nc.vector.tensor_copy(
+        nc.scalar.copy(
             out=x_grouped[:].bitcast(F32).rearrange("p (c u) -> p c u", u=2),
             in_=xT_ps[:].rearrange("p u c -> p c u"),
         )
@@ -160,9 +160,7 @@ def tile_deter_pb_s_kernel(tc, hid0, deter, hw1, hb1, hg1, gw, gb, out):
 
         nc.tensor.transpose(vecT_ps[:], vec_rows[:], ident_bf[:])
         vec = keep.tile([P, VEC_COLS], F32, name="vec")
-        nc.vector.tensor_copy(out=vec[:], in_=vecT_ps[:, 0:VEC_COLS])
-        z_bias = vec[:, GB_COL:VEC_COLS].rearrange("p (j g m) -> p j g m", j=BLOCKS, g=GATES)[:, :, Z_GATE, :]
-        nc.vector.tensor_scalar(out=z_bias, in0=z_bias, scalar1=-1.0, scalar2=None, op0=ALU.add)
+        nc.scalar.copy(out=vec[:], in_=vecT_ps[:, 0:VEC_COLS])
         nc.vector.quantize_mx(out=x_codes[:].bitcast(FP8X4), scales=x_scales[:], in_=x_grouped[:])
 
         def vec_col(first, c):
@@ -223,6 +221,8 @@ def tile_deter_pb_s_kernel(tc, hid0, deter, hw1, hb1, hg1, gw, gb, out):
         regroup(("w1", 1), WHOLE)
         quantise(("w1", 1), WHOLE)
         multiply(("w1", 1), WHOLE, u_ps[1], x_codes, x_scales)
+        z_bias = vec[:, GB_COL:VEC_COLS].rearrange("p (j g m) -> p j g m", j=BLOCKS, g=GATES)[:, :, Z_GATE, :]
+        nc.vector.tensor_scalar(out=z_bias, in0=z_bias, scalar1=-1.0, scalar2=None, op0=ALU.add)
         regroup((R_GATE, 0), WHOLE)
         squares(0)
         squares(1)

@@ -120,48 +120,46 @@ def tile_deter_pb_s_kernel(tc, hid0, deter, hw1, hb1, hg1, gw, gb, out):
         d_tok = keep.tile([P, BLOCKS * PAIRS, P], BF16, name="d_tok")
         deter_view = deter.rearrange("b (q h f) -> h b q f", h=2, f=P)
         out_view = out.rearrange("b (q h f) -> h b q f", h=2, f=P)
-        for j in range(BLOCKS):
-            nc.sync.dma_start(out=x_sb[j * B : (j + 1) * B, :], in_=hid0[:, j * DPB : (j + 1) * DPB])
-        load_weights(("w1", 0), FIRST_HALF)
-        load_weights(("w1", 0), SECOND_HALF)
+        nc.sync.dma_start(out=x_sb[:], in_=hid0.rearrange("b (j k) -> (b j) k", j=BLOCKS))
+        load_weights(("w1", 0), WHOLE)
+        load_weights(("w1", 1), WHOLE)
         nc.sync.dma_start(out=vec_rows[HB_COL:HG_COL, :], in_=hb1.rearrange("(r p) -> r p", p=P))
         nc.sync.dma_start(out=vec_rows[HG_COL:GB_COL, :], in_=hg1.rearrange("(r p) -> r p", p=P))
-        nc.sync.dma_start(out=vec_rows[GB_COL:VEC_COLS, :], in_=gb.rearrange("(r p) -> r p", p=P))
-        load_weights(("w1", 1), WHOLE)
+        gb_rows = gb.rearrange("(r p) -> r p", p=P)
+        nc.sync.dma_start(out=vec_rows[GB_COL : GB_COL + 16, :], in_=gb_rows[0:16, :])
+        nc.sync.dma_start(out=vec_rows[GB_COL + 16 : VEC_COLS, :], in_=gb_rows[16 : VEC_COLS - GB_COL, :])
         for g in range(GATES):
             load_weights((g, 0), WHOLE)
-        for h in range(2):
-            nc.sync.dma_start(out=d_tok[h * B : (h + 1) * B, :, :], in_=deter_view[h])
         load_weights((R_GATE, 1), WHOLE)
         load_weights((C_GATE, 1), WHOLE)
         load_weights((Z_GATE, 1), FIRST_HALF)
         load_weights((Z_GATE, 1), SECOND_HALF)
+        for h in range(2):
+            nc.sync.dma_start(out=d_tok[h * B : (h + 1) * B, :, :], in_=deter_view[h])
 
         xT_ps = psum.tile([P, 2, P], F32, name="xT_ps", tag="bank_0")
         vecT_ps = psum.tile([P, P], BF16, name="vecT_ps", tag="bank_1")
         dT_ps = psum.tile([P, BLOCKS, CHUNKS, B], BF16, name="dT_ps", tag="bank_2")
         u_ps = [psum.tile([P, CHUNKS, B], F32, name="u_ps_%d" % j, tag="bank_%d" % (3 + j)) for j in range(BLOCKS)]
 
-        regroup(("w1", 0), FIRST_HALF)
-        regroup(("w1", 0), SECOND_HALF)
-        quantise(("w1", 0), FIRST_HALF)
-        quantise(("w1", 0), SECOND_HALF)
-
         x_words = x_sb[:].bitcast(F32).rearrange("p (w u) -> p u w", u=2)
         for u in range(2):
             nc.tensor.transpose(xT_ps[:, u, :], x_words[:, u, :], ident_f32[:])
         x_grouped = keep.tile([P, P * PACK], BF16, name="x_grouped", align_bytes=64)
         nc.scalar.copy(
-            out=x_grouped[:].bitcast(F32).rearrange("p (c u) -> p c u", u=2),
-            in_=xT_ps[:].rearrange("p u c -> p c u"),
+            out=x_grouped[:].bitcast(F32).rearrange("p (j b u) -> p j b u", j=BLOCKS, u=2),
+            in_=xT_ps[:].rearrange("p u (b j) -> p j b u", j=BLOCKS),
         )
         x_codes = keep.tile([P, P], U32, name="x_codes", align_bytes=64)
         x_scales = keep.tile([P, P], U8, name="x_scales", align_bytes=64)
-
+        regroup(("w1", 0), WHOLE)
+        nc.vector.quantize_mx(out=x_codes[:].bitcast(FP8X4), scales=x_scales[:], in_=x_grouped[:])
+        regroup(("w1", 1), WHOLE)
+        quantise(("w1", 0), WHOLE)
+        quantise(("w1", 1), WHOLE)
         nc.tensor.transpose(vecT_ps[:], vec_rows[:], ident_bf[:])
         vec = keep.tile([P, VEC_COLS], F32, name="vec")
         nc.scalar.copy(out=vec[:], in_=vecT_ps[:, 0:VEC_COLS])
-        nc.vector.quantize_mx(out=x_codes[:].bitcast(FP8X4), scales=x_scales[:], in_=x_grouped[:])
 
         def vec_col(first, c):
             return vec[:, first + c : first + c + 1]
@@ -169,8 +167,8 @@ def tile_deter_pb_s_kernel(tc, hid0, deter, hw1, hb1, hg1, gw, gb, out):
         sq = keep.tile([P, BLOCKS, CHUNKS, B], F32, name="sq")
         sq_sum = keep.tile([P, BLOCKS, B], F32, name="sq_sum")
         gained = keep.tile([P, BLOCKS, CHUNKS, B], F32, name="gained")
-        normed = keep.tile([P, BLOCKS, CHUNKS, B], F32, name="normed")
-        gate_h = keep.tile([P, BLOCKS, CHUNKS, B], F32, name="gate_h")
+        normed = keep.tile([P, BLOCKS, B, PACK], F32, name="normed")
+        gate_h = keep.tile([P, BLOCKS, B, PACK], F32, name="gate_h")
         h_grouped = keep.tile([P, BLOCKS, B, PACK], BF16, name="h_grouped", align_bytes=64)
         h_codes = keep.tile([P, P], U32, name="h_codes", align_bytes=64)
         h_scales = keep.tile([P, P], U8, name="h_scales", align_bytes=64)
@@ -202,52 +200,49 @@ def tile_deter_pb_s_kernel(tc, hid0, deter, hw1, hb1, hg1, gw, gb, out):
 
         def normalise(j):
             nc.vector.tensor_tensor(
-                out=normed[:, j], in0=gained[:, j], in1=rstd[:].unsqueeze(1).to_broadcast([P, CHUNKS, B]), op=ALU.mult
+                out=normed[:, j], in0=gained[:, j].rearrange("p t b -> p b t"),
+                in1=rstd[:].unsqueeze(2).to_broadcast([P, B, PACK]), op=ALU.mult,
             )
 
         def silu_gate(j):
             nc.scalar.activation(
-                out=gate_h[:, j].rearrange("p t b -> p (t b)"), in_=normed[:, j].rearrange("p t b -> p (t b)"),
+                out=gate_h[:, j].rearrange("p b t -> p (b t)"), in_=normed[:, j].rearrange("p b t -> p (b t)"),
                 func=ACT.Sigmoid,
             )
 
         def silu_product(j):
-            nc.vector.tensor_tensor(
-                out=h_grouped[:, j], in0=normed[:, j].rearrange("p t b -> p b t"),
-                in1=gate_h[:, j].rearrange("p t b -> p b t"), op=ALU.mult,
-            )
+            nc.vector.tensor_tensor(out=h_grouped[:, j], in0=normed[:, j], in1=gate_h[:, j], op=ALU.mult)
 
         multiply(("w1", 0), WHOLE, u_ps[0], x_codes, x_scales)
-        regroup(("w1", 1), WHOLE)
-        quantise(("w1", 1), WHOLE)
         multiply(("w1", 1), WHOLE, u_ps[1], x_codes, x_scales)
+        regroup((R_GATE, 0), WHOLE)
         z_bias = vec[:, GB_COL:VEC_COLS].rearrange("p (j g m) -> p j g m", j=BLOCKS, g=GATES)[:, :, Z_GATE, :]
         nc.vector.tensor_scalar(out=z_bias, in0=z_bias, scalar1=-1.0, scalar2=None, op0=ALU.add)
-        regroup((R_GATE, 0), WHOLE)
+        regroup_on_vector((C_GATE, 0), WHOLE)
         squares(0)
-        squares(1)
-        regroup((C_GATE, 0), WHOLE)
-        quantise((R_GATE, 0), WHOLE)
         mean_of_squares(0)
-        regroup((Z_GATE, 0), WHOLE)
+        quantise((R_GATE, 0), WHOLE)
+        squares(1)
         mean_of_squares(1)
-        quantise((C_GATE, 0), WHOLE)
+        regroup_on_scalar((C_GATE, 0), WHOLE)
+        regroup((Z_GATE, 0), WHOLE)
         bias_and_gain(0)
         bias_and_gain(1)
+        quantise((C_GATE, 0), WHOLE)
         nc.scalar.activation(out=rstd[:], in_=mean_ps[:], func=ACT.Abs_reciprocal_sqrt, bias=eps_col[:], scale=1.0)
         nc.scalar.activation(out=warm_col[:, 1:2], in_=one_col[:], func=ACT.Sigmoid)
         for j in range(BLOCKS):
             normalise(j)
             silu_gate(j)
         quantise((Z_GATE, 0), WHOLE)
+        regroup((R_GATE, 1), WHOLE)
         for j in range(BLOCKS):
             silu_product(j)
-        nc.vector.quantize_mx(
-            out=h_codes[:].bitcast(FP8X4), scales=h_scales[:], in_=h_grouped[:].rearrange("p j b t -> p (j b t)")
-        )
-        for q in range(BLOCKS * PAIRS):
-            nc.tensor.transpose(
-                dT_ps[:].rearrange("p j m b -> p (j m b)")[:, q * P : (q + 1) * P], d_tok[:, q, :], ident_bf[:]
+        for j in range(BLOCKS):
+            nc.vector.quantize_mx(
+                out=h_codes[:, j * B : (j + 1) * B].bitcast(FP8X4),
+                scales=h_scales[:, j * B : (j + 1) * B],
+                in_=h_grouped[:, j].rearrange("p b t -> p (b t)"),
             )
 
         gate_ps = {}
@@ -316,28 +311,30 @@ def tile_deter_pb_s_kernel(tc, hid0, deter, hw1, hb1, hg1, gw, gb, out):
                     out=out_view[h][:, j * PAIRS : (j + 1) * PAIRS, :], in_=result[h * B : (h + 1) * B, j, :, :]
                 )
 
-        regroup((R_GATE, 1), WHOLE)
-        quantise((R_GATE, 1), WHOLE)
         regroup((C_GATE, 1), WHOLE)
-        quantise((C_GATE, 1), WHOLE)
-        gate_product((R_GATE, 0), WHOLE)
-        gate_product((C_GATE, 0), WHOLE)
+        quantise((R_GATE, 1), WHOLE)
+        for g in range(GATES):
+            gate_product((g, 0), WHOLE)
         gate_product((R_GATE, 1), WHOLE)
-        gate_product((Z_GATE, 0), WHOLE)
+        regroup_on_vector((Z_GATE, 1), FIRST_HALF)
+        quantise((C_GATE, 1), WHOLE)
         gate_product((C_GATE, 1), WHOLE)
-        regroup((Z_GATE, 1), FIRST_HALF)
+        for q in range(BLOCKS * PAIRS):
+            nc.tensor.transpose(
+                dT_ps[:].rearrange("p j m b -> p (j m b)")[:, q * P : (q + 1) * P], d_tok[:, q, :], ident_bf[:]
+            )
         sigmoid_gate((R_GATE, 0), WHOLE, reset)
         reset_candidate(0)
-        quantise((Z_GATE, 1), FIRST_HALF)
+        regroup_on_scalar((Z_GATE, 1), FIRST_HALF)
         regroup((Z_GATE, 1), SECOND_HALF)
+        quantise((Z_GATE, 1), FIRST_HALF)
         quantise((Z_GATE, 1), SECOND_HALF)
         gate_product((Z_GATE, 1), FIRST_HALF)
         gate_product((Z_GATE, 1), SECOND_HALF)
-
         sigmoid_gate((R_GATE, 1), WHOLE, reset)
+        reset_candidate(1)
         candidate(0)
         difference(0)
-        reset_candidate(1)
         sigmoid_gate((Z_GATE, 0), WHOLE, update)
         for q in range(PAIRS):
             weighted_step(0, q)

@@ -120,8 +120,8 @@ def tile_deter_pb_s_kernel(tc, hid0, deter, hw1, hb1, hg1, gw, gb, out):
         d_tok = keep.tile([P, BLOCKS * PAIRS, P], BF16, name="d_tok")
         deter_view = deter.rearrange("b (q h f) -> h b q f", h=2, f=P)
         out_view = out.rearrange("b (q h f) -> h b q f", h=2, f=P)
-        nc.sync.dma_start(out=x_sb[:], in_=hid0.rearrange("b (j k) -> (b j) k", j=BLOCKS))
         load_weights(("w1", 0), WHOLE)
+        nc.sync.dma_start(out=x_sb[:], in_=hid0.rearrange("b (j k) -> (b j) k", j=BLOCKS))
         load_weights(("w1", 1), WHOLE)
         nc.sync.dma_start(out=vec_rows[HB_COL:HG_COL, :], in_=hb1.rearrange("(r p) -> r p", p=P))
         nc.sync.dma_start(out=vec_rows[HG_COL:GB_COL, :], in_=hg1.rearrange("(r p) -> r p", p=P))
@@ -145,6 +145,7 @@ def tile_deter_pb_s_kernel(tc, hid0, deter, hw1, hb1, hg1, gw, gb, out):
         x_words = x_sb[:].bitcast(F32).rearrange("p (w u) -> p u w", u=2)
         for u in range(2):
             nc.tensor.transpose(xT_ps[:, u, :], x_words[:, u, :], ident_f32[:])
+        regroup(("w1", 0), WHOLE)
         x_grouped = keep.tile([P, P * PACK], BF16, name="x_grouped", align_bytes=64)
         nc.scalar.copy(
             out=x_grouped[:].bitcast(F32).rearrange("p (j b u) -> p j b u", j=BLOCKS, u=2),
@@ -152,10 +153,9 @@ def tile_deter_pb_s_kernel(tc, hid0, deter, hw1, hb1, hg1, gw, gb, out):
         )
         x_codes = keep.tile([P, P], U32, name="x_codes", align_bytes=64)
         x_scales = keep.tile([P, P], U8, name="x_scales", align_bytes=64)
-        regroup(("w1", 0), WHOLE)
-        nc.vector.quantize_mx(out=x_codes[:].bitcast(FP8X4), scales=x_scales[:], in_=x_grouped[:])
-        regroup(("w1", 1), WHOLE)
         quantise(("w1", 0), WHOLE)
+        regroup(("w1", 1), WHOLE)
+        nc.vector.quantize_mx(out=x_codes[:].bitcast(FP8X4), scales=x_scales[:], in_=x_grouped[:])
         quantise(("w1", 1), WHOLE)
         nc.tensor.transpose(vecT_ps[:], vec_rows[:], ident_bf[:])
         vec = keep.tile([P, VEC_COLS], F32, name="vec")
@@ -217,7 +217,7 @@ def tile_deter_pb_s_kernel(tc, hid0, deter, hw1, hb1, hg1, gw, gb, out):
         multiply(("w1", 1), WHOLE, u_ps[1], x_codes, x_scales)
         regroup((R_GATE, 0), WHOLE)
         z_bias = vec[:, GB_COL:VEC_COLS].rearrange("p (j g m) -> p j g m", j=BLOCKS, g=GATES)[:, :, Z_GATE, :]
-        nc.vector.tensor_scalar(out=z_bias, in0=z_bias, scalar1=-1.0, scalar2=None, op0=ALU.add)
+        nc.vector.tensor_scalar(out=z_bias, in0=z_bias, scalar1=-1.0, scalar2=1.0, op0=ALU.mult, op1=ALU.add)
         regroup_on_vector((C_GATE, 0), WHOLE)
         squares(0)
         mean_of_squares(0)
@@ -255,23 +255,29 @@ def tile_deter_pb_s_kernel(tc, hid0, deter, hw1, hb1, hg1, gw, gb, out):
 
         reset = keep.tile([P, BLOCKS, CHUNKS, B], F32, name="reset")
         rc = keep.tile([P, BLOCKS, CHUNKS, B], F32, name="rc")
-        cand = keep.tile([P, BLOCKS, CHUNKS, B], F32, name="cand")
-        diff = keep.tile([P, BLOCKS, CHUNKS, B], F32, name="diff")
-        update = keep.tile([P, BLOCKS, CHUNKS, B], F32, name="update")
-        step = keep.tile([P, BLOCKS, CHUNKS, B], F32, name="step")
+        minus_cand = keep.tile([P, BLOCKS, CHUNKS, B], F32, name="minus_cand")
+        stay = keep.tile([P, BLOCKS, CHUNKS, B], F32, name="stay")
+        old = keep.tile([P, BLOCKS, CHUNKS, B], F32, name="old")
+        new = keep.tile([P, BLOCKS, CHUNKS, B], F32, name="new")
         result = keep.tile([P, BLOCKS, PAIRS, P], F32, name="result")
-        stepT_ps = {}
+        sum_ps = {}
 
         def gate_product(key, cols):
             multiply(key, cols, gate_ps[key], h_codes, h_scales)
 
-        def sigmoid_gate(key, cols, dest):
+        def sigmoid_gate(key, cols, dest, scale):
             g, j = key
             for m in range(cols[0] // P, cols[1] // P):
                 nc.scalar.activation(
                     out=dest[:, j, m, :], in_=gate_ps[key][:, m, :], func=ACT.Sigmoid,
-                    bias=vec_col(GB_COL, (j * GATES + g) * CHUNKS + m), scale=1.0,
+                    bias=vec_col(GB_COL, (j * GATES + g) * CHUNKS + m), scale=scale,
                 )
+
+        def reset_gate(j):
+            sigmoid_gate((R_GATE, j), WHOLE, reset, 1.0)
+
+        def keep_gate(j, cols):
+            sigmoid_gate((Z_GATE, j), cols, stay, -1.0)
 
         def reset_candidate(j):
             for m in range(CHUNKS):
@@ -283,27 +289,33 @@ def tile_deter_pb_s_kernel(tc, hid0, deter, hw1, hb1, hg1, gw, gb, out):
 
         def candidate(j):
             nc.scalar.activation(
-                out=cand[:, j].rearrange("p m b -> p (m b)"), in_=rc[:, j].rearrange("p m b -> p (m b)"), func=ACT.Tanh
+                out=minus_cand[:, j].rearrange("p m b -> p (m b)"), in_=rc[:, j].rearrange("p m b -> p (m b)"),
+                func=ACT.Tanh, scale=-1.0,
             )
 
-        def difference(j):
-            nc.vector.tensor_tensor(out=diff[:, j], in0=cand[:, j], in1=dT_ps[:, j], op=ALU.subtract)
+        def old_part(j, lo, hi):
+            nc.vector.tensor_tensor(out=old[:, j, lo:hi, :], in0=stay[:, j, lo:hi, :], in1=dT_ps[:, j, lo:hi, :], op=ALU.mult)
 
-        def weighted_step(j, q):
-            pair = slice(2 * q, 2 * q + 2)
-            nc.vector.tensor_tensor(out=step[:, j, pair, :], in0=update[:, j, pair, :], in1=diff[:, j, pair, :], op=ALU.mult)
-
-        def to_tokens(j, q):
-            bank = 3 + j if q == 0 else j
-            stepT_ps[(j, q)] = psum.tile([P, P], F32, name="stepT_ps_%d_%d" % (j, q), tag="bank_%d" % bank)
-            nc.tensor.transpose(
-                stepT_ps[(j, q)][:], step[:, j, 2 * q : 2 * q + 2, :].rearrange("p m b -> p (m b)"), ident_f32[:]
+        def new_part(j, lo, hi):
+            nc.vector.scalar_tensor_tensor(
+                out=new[:, j, lo:hi, :], in0=stay[:, j, lo:hi, :], scalar=1.0, in1=minus_cand[:, j, lo:hi, :],
+                op0=ALU.subtract, op1=ALU.mult,
             )
 
-        def add_state(j, q):
-            nc.vector.tensor_tensor(
-                out=result[:, j, q, :], in0=stepT_ps[(j, q)][:], in1=d_tok[:, j * PAIRS + q, :], op=ALU.add
+        def to_tokens(part, j, q, first):
+            if first:
+                bank = 3 + j if q == 0 else j
+                sum_ps[(j, q)] = psum.tile([P, P], F32, name="sum_ps_%d_%d" % (j, q), tag="bank_%d" % bank)
+            nc.tensor.matmul(
+                out=sum_ps[(j, q)][:], lhsT=part[:, j, 2 * q : 2 * q + 2, :].rearrange("p m b -> p (m b)"),
+                rhs=ident_f32[:], start=first, stop=not first, is_transpose=True,
             )
+
+        def new_state_on_scalar(j, q):
+            nc.scalar.copy(out=result[:, j, q, :], in_=sum_ps[(j, q)][:])
+
+        def new_state_on_vector(j, q):
+            nc.vector.tensor_copy(out=result[:, j, q, :], in_=sum_ps[(j, q)][:])
 
         def store(j):
             for h in range(2):
@@ -323,7 +335,7 @@ def tile_deter_pb_s_kernel(tc, hid0, deter, hw1, hb1, hg1, gw, gb, out):
             nc.tensor.transpose(
                 dT_ps[:].rearrange("p j m b -> p (j m b)")[:, q * P : (q + 1) * P], d_tok[:, q, :], ident_bf[:]
             )
-        sigmoid_gate((R_GATE, 0), WHOLE, reset)
+        reset_gate(0)
         reset_candidate(0)
         regroup_on_scalar((Z_GATE, 1), FIRST_HALF)
         regroup((Z_GATE, 1), SECOND_HALF)
@@ -331,22 +343,26 @@ def tile_deter_pb_s_kernel(tc, hid0, deter, hw1, hb1, hg1, gw, gb, out):
         quantise((Z_GATE, 1), SECOND_HALF)
         gate_product((Z_GATE, 1), FIRST_HALF)
         gate_product((Z_GATE, 1), SECOND_HALF)
-        sigmoid_gate((R_GATE, 1), WHOLE, reset)
+        reset_gate(1)
         reset_candidate(1)
         candidate(0)
-        difference(0)
-        sigmoid_gate((Z_GATE, 0), WHOLE, update)
+        keep_gate(0, WHOLE)
+        old_part(0, 0, CHUNKS)
+        new_part(0, 0, CHUNKS)
         for q in range(PAIRS):
-            weighted_step(0, q)
-            to_tokens(0, q)
+            to_tokens(old, 0, q, True)
+            to_tokens(new, 0, q, False)
         candidate(1)
-        difference(1)
-        sigmoid_gate((Z_GATE, 1), FIRST_HALF, update)
-        sigmoid_gate((Z_GATE, 1), SECOND_HALF, update)
+        keep_gate(1, FIRST_HALF)
+        keep_gate(1, SECOND_HALF)
         for q in range(PAIRS):
-            weighted_step(1, q)
-            to_tokens(1, q)
-        for j in range(BLOCKS):
-            for q in range(PAIRS):
-                add_state(j, q)
-            store(j)
+            new_state_on_scalar(0, q)
+        store(0)
+        for q in range(PAIRS):
+            old_part(1, 2 * q, 2 * q + 2)
+            new_part(1, 2 * q, 2 * q + 2)
+            to_tokens(old, 1, q, True)
+            to_tokens(new, 1, q, False)
+        new_state_on_scalar(1, 0)
+        new_state_on_vector(1, 1)
+        store(1)

@@ -117,8 +117,7 @@ def tile_deter_pb_s_kernel(tc, hid0, deter, hw1, hb1, hg1, gw, gb, out):
         nc.vector.memset(eps_col[:], EPS)
 
         x_sb = keep.tile([P, DPB], BF16, name="x_sb")
-        d_tok = keep.tile([P, BLOCKS * PAIRS, P], BF16, name="d_tok")
-        deter_view = deter.rearrange("b (q h f) -> h b q f", h=2, f=P)
+        d_sb = keep.tile([P, DPB], BF16, name="d_sb")
         out_view = out.rearrange("b (q h f) -> h b q f", h=2, f=P)
         load_weights(("w1", 0), WHOLE)
         nc.sync.dma_start(out=x_sb[:], in_=hid0.rearrange("b (j k) -> (b j) k", j=BLOCKS))
@@ -128,18 +127,18 @@ def tile_deter_pb_s_kernel(tc, hid0, deter, hw1, hb1, hg1, gw, gb, out):
         gb_rows = gb.rearrange("(r p) -> r p", p=P)
         nc.sync.dma_start(out=vec_rows[GB_COL : GB_COL + 16, :], in_=gb_rows[0:16, :])
         nc.sync.dma_start(out=vec_rows[GB_COL + 16 : VEC_COLS, :], in_=gb_rows[16 : VEC_COLS - GB_COL, :])
-        for g in range(GATES):
-            load_weights((g, 0), WHOLE)
+        load_weights((R_GATE, 0), WHOLE)
+        load_weights((C_GATE, 0), WHOLE)
+        nc.sync.dma_start(out=d_sb[:], in_=deter.rearrange("b (j k) -> (b j) k", j=BLOCKS))
+        load_weights((Z_GATE, 0), WHOLE)
         load_weights((R_GATE, 1), WHOLE)
         load_weights((C_GATE, 1), WHOLE)
         load_weights((Z_GATE, 1), FIRST_HALF)
         load_weights((Z_GATE, 1), SECOND_HALF)
-        for h in range(2):
-            nc.sync.dma_start(out=d_tok[h * B : (h + 1) * B, :, :], in_=deter_view[h])
 
         xT_ps = psum.tile([P, 2, P], F32, name="xT_ps", tag="bank_0")
         vecT_ps = psum.tile([P, P], BF16, name="vecT_ps", tag="bank_1")
-        dT_ps = psum.tile([P, BLOCKS, CHUNKS, B], BF16, name="dT_ps", tag="bank_2")
+        dT_ps = psum.tile([P, CHUNKS, P], BF16, name="dT_ps", tag="bank_2")
         u_ps = [psum.tile([P, CHUNKS, B], F32, name="u_ps_%d" % j, tag="bank_%d" % (3 + j)) for j in range(BLOCKS)]
 
         x_words = x_sb[:].bitcast(F32).rearrange("p (w u) -> p u w", u=2)
@@ -245,14 +244,18 @@ def tile_deter_pb_s_kernel(tc, hid0, deter, hw1, hb1, hg1, gw, gb, out):
                 in_=h_grouped[:, j].rearrange("p b t -> p (b t)"),
             )
 
+        for m in range(CHUNKS):
+            nc.tensor.transpose(dT_ps[:, m, :], d_sb[:, m * P : (m + 1) * P], ident_bf[:])
+        d_feat = dT_ps[:].rearrange("p m (b j) -> p j m b", j=BLOCKS)
+
         gate_ps = {}
         for j in range(BLOCKS):
             gate_ps[(R_GATE, j)] = psum.tile([P, CHUNKS, B], F32, name="r_ps_%d" % j, tag="bank_%d" % (3 + j))
         gate_ps[(C_GATE, 0)] = psum.tile([P, CHUNKS, B], F32, name="c_ps_0", tag="bank_1")
         gate_ps[(C_GATE, 1)] = psum.tile([P, CHUNKS, B], F32, name="c_ps_1", tag="bank_5")
         gate_ps[(Z_GATE, 0)] = psum.tile([P, CHUNKS, B], F32, name="z_ps_0", tag="bank_6")
-        gate_ps[(Z_GATE, 1)] = psum.tile([P, CHUNKS, B], F32, name="z_ps_1", tag="bank_7")
 
+        spare_ps = psum.tile([P, DPB], F32, name="spare_ps", tag="bank_7")
         reset = keep.tile([P, BLOCKS, CHUNKS, B], F32, name="reset")
         rc = keep.tile([P, BLOCKS, CHUNKS, B], F32, name="rc")
         minus_cand = keep.tile([P, BLOCKS, CHUNKS, B], F32, name="minus_cand")
@@ -261,6 +264,17 @@ def tile_deter_pb_s_kernel(tc, hid0, deter, hw1, hb1, hg1, gw, gb, out):
         new = keep.tile([P, BLOCKS, CHUNKS, B], F32, name="new")
         result = keep.tile([P, BLOCKS, PAIRS, P], F32, name="result")
         sum_ps = {}
+
+        def keep_clock(key):
+            nc.tensor.matmul_mx(
+                out=spare_ps[:],
+                lhsT=codes[key][:, 0:P].bitcast(FP8X4),
+                lhsT_scale=scales[key][:, 0:P],
+                rhs=codes[key][:].bitcast(FP8X4),
+                rhs_scale=scales[key][:],
+                start=True,
+                stop=True,
+            )
 
         def gate_product(key, cols):
             multiply(key, cols, gate_ps[key], h_codes, h_scales)
@@ -294,7 +308,7 @@ def tile_deter_pb_s_kernel(tc, hid0, deter, hw1, hb1, hg1, gw, gb, out):
             )
 
         def old_part(j, lo, hi):
-            nc.vector.tensor_tensor(out=old[:, j, lo:hi, :], in0=stay[:, j, lo:hi, :], in1=dT_ps[:, j, lo:hi, :], op=ALU.mult)
+            nc.vector.tensor_tensor(out=old[:, j, lo:hi, :], in0=stay[:, j, lo:hi, :], in1=d_feat[:, j, lo:hi, :], op=ALU.mult)
 
         def new_part(j, lo, hi):
             nc.vector.scalar_tensor_tensor(
@@ -325,44 +339,44 @@ def tile_deter_pb_s_kernel(tc, hid0, deter, hw1, hb1, hg1, gw, gb, out):
 
         regroup((C_GATE, 1), WHOLE)
         quantise((R_GATE, 1), WHOLE)
-        for g in range(GATES):
-            gate_product((g, 0), WHOLE)
-        gate_product((R_GATE, 1), WHOLE)
-        regroup_on_vector((Z_GATE, 1), FIRST_HALF)
+        for key in ((C_GATE, 0), (C_GATE, 0), (Z_GATE, 0), (Z_GATE, 0)):
+            keep_clock(key)
+        for key in ((R_GATE, 0), (C_GATE, 0), (R_GATE, 1)):
+            gate_product(key, WHOLE)
+        gate_product((Z_GATE, 0), WHOLE)
+        regroup((Z_GATE, 1), FIRST_HALF)
         quantise((C_GATE, 1), WHOLE)
         gate_product((C_GATE, 1), WHOLE)
-        for q in range(BLOCKS * PAIRS):
-            nc.tensor.transpose(
-                dT_ps[:].rearrange("p j m b -> p (j m b)")[:, q * P : (q + 1) * P], d_tok[:, q, :], ident_bf[:]
-            )
-        reset_gate(0)
-        reset_candidate(0)
-        regroup_on_scalar((Z_GATE, 1), FIRST_HALF)
         regroup((Z_GATE, 1), SECOND_HALF)
         quantise((Z_GATE, 1), FIRST_HALF)
-        quantise((Z_GATE, 1), SECOND_HALF)
+        gate_ps[(Z_GATE, 1)] = psum.tile([P, CHUNKS, B], F32, name="z_ps_1", tag="bank_7")
         gate_product((Z_GATE, 1), FIRST_HALF)
+        quantise((Z_GATE, 1), SECOND_HALF)
         gate_product((Z_GATE, 1), SECOND_HALF)
+        reset_gate(0)
+        reset_candidate(0)
         reset_gate(1)
         reset_candidate(1)
-        candidate(0)
         keep_gate(0, WHOLE)
+        candidate(0)
+        keep_gate(1, FIRST_HALF)
+        keep_gate(1, SECOND_HALF)
+        candidate(1)
         old_part(0, 0, CHUNKS)
         new_part(0, 0, CHUNKS)
         for q in range(PAIRS):
             to_tokens(old, 0, q, True)
+        for q in range(PAIRS):
             to_tokens(new, 0, q, False)
-        candidate(1)
-        keep_gate(1, FIRST_HALF)
-        keep_gate(1, SECOND_HALF)
+        old_part(1, 0, CHUNKS)
+        for q in range(PAIRS):
+            to_tokens(old, 1, q, True)
+        for q in range(PAIRS):
+            new_part(1, 2 * q, 2 * q + 2)
+            to_tokens(new, 1, q, False)
         for q in range(PAIRS):
             new_state_on_scalar(0, q)
         store(0)
-        for q in range(PAIRS):
-            old_part(1, 2 * q, 2 * q + 2)
-            new_part(1, 2 * q, 2 * q + 2)
-            to_tokens(old, 1, q, True)
-            to_tokens(new, 1, q, False)
         new_state_on_scalar(1, 0)
         new_state_on_vector(1, 1)
         store(1)

@@ -331,9 +331,9 @@ def tile_deter_pb_s_kernel(tc, hid0, deter, hw1, hb1, hg1, gw, gb, out):
         def new_state_on_vector(j, q):
             nc.vector.tensor_copy(out=result[:, j, q, :], in_=sum_ps[(j, q)][:])
 
-        def store(j):
-            for h in range(2):
-                nc.sync.dma_start(
+        def store(j, engines):
+            for h, engine in enumerate(engines):
+                engine.dma_start(
                     out=out_view[h][:, j * PAIRS : (j + 1) * PAIRS, :], in_=result[h * B : (h + 1) * B, j, :, :]
                 )
 
@@ -376,7 +376,7 @@ def tile_deter_pb_s_kernel(tc, hid0, deter, hw1, hb1, hg1, gw, gb, out):
             to_tokens(new, 1, q, False)
         for q in range(PAIRS):
             new_state_on_scalar(0, q)
-        store(0)
+        store(0, (nc.sync, nc.sync))
         new_state_on_scalar(1, 0)
         new_state_on_vector(1, 1)
-        store(1)
+        store(1, (nc.sync, nc.scalar))

@@ -101,6 +101,9 @@ def tile_deter_pb_s_kernel(tc, hid0, deter, hw1, hb1, hg1, gw, gb, out):
                     stop=True,
                 )
 
+        def spot(m):
+            return m % PAIRS * 2 + m // PAIRS
+
         ident_f32 = keep.tile([P, P], F32, name="ident_f32")
         make_identity(nc, ident_f32[:])
         ident_bf = keep.tile([P, P], BF16, name="ident_bf")
@@ -118,7 +121,7 @@ def tile_deter_pb_s_kernel(tc, hid0, deter, hw1, hb1, hg1, gw, gb, out):
 
         x_sb = keep.tile([P, DPB], BF16, name="x_sb")
         d_sb = keep.tile([P, DPB], BF16, name="d_sb")
-        out_view = out.rearrange("b (q h f) -> h b q f", h=2, f=P)
+        out_view = out.rearrange("b (j h q f) -> h b j q f", j=BLOCKS, h=2, f=P)
         load_weights(("w1", 0), WHOLE)
         nc.sync.dma_start(out=x_sb[:], in_=hid0.rearrange("b (j k) -> (b j) k", j=BLOCKS))
         load_weights(("w1", 1), WHOLE)
@@ -245,7 +248,7 @@ def tile_deter_pb_s_kernel(tc, hid0, deter, hw1, hb1, hg1, gw, gb, out):
             )
 
         for m in range(CHUNKS):
-            nc.tensor.transpose(dT_ps[:, m, :], d_sb[:, m * P : (m + 1) * P], ident_bf[:])
+            nc.tensor.transpose(dT_ps[:, spot(m), :], d_sb[:, m * P : (m + 1) * P], ident_bf[:])
         d_feat = dT_ps[:].rearrange("p m (b j) -> p j m b", j=BLOCKS)
 
         gate_ps = {}
@@ -283,7 +286,7 @@ def tile_deter_pb_s_kernel(tc, hid0, deter, hw1, hb1, hg1, gw, gb, out):
             g, j = key
             for m in range(cols[0] // P, cols[1] // P):
                 nc.scalar.activation(
-                    out=dest[:, j, m, :], in_=gate_ps[key][:, m, :], func=ACT.Sigmoid,
+                    out=dest[:, j, spot(m), :], in_=gate_ps[key][:, m, :], func=ACT.Sigmoid,
                     bias=vec_col(GB_COL, (j * GATES + g) * CHUNKS + m), scale=scale,
                 )
 
@@ -296,9 +299,9 @@ def tile_deter_pb_s_kernel(tc, hid0, deter, hw1, hb1, hg1, gw, gb, out):
         def reset_candidate(j):
             for m in range(CHUNKS):
                 nc.vector.scalar_tensor_tensor(
-                    out=rc[:, j, m, :], in0=gate_ps[(C_GATE, j)][:, m, :],
+                    out=rc[:, j, spot(m), :], in0=gate_ps[(C_GATE, j)][:, m, :],
                     scalar=vec_col(GB_COL, (j * GATES + C_GATE) * CHUNKS + m),
-                    in1=reset[:, j, m, :], op0=ALU.add, op1=ALU.mult,
+                    in1=reset[:, j, spot(m), :], op0=ALU.add, op1=ALU.mult,
                 )
 
         def candidate(j):
@@ -334,7 +337,7 @@ def tile_deter_pb_s_kernel(tc, hid0, deter, hw1, hb1, hg1, gw, gb, out):
         def store(j, engines):
             for h, engine in enumerate(engines):
                 engine.dma_start(
-                    out=out_view[h][:, j * PAIRS : (j + 1) * PAIRS, :], in_=result[h * B : (h + 1) * B, j, :, :]
+                    out=out_view[h][:, j], in_=result[h * B : (h + 1) * B, j, :, :]
                 )
 
         regroup((C_GATE, 1), WHOLE)

import concourse.mybir as mybir
from concourse.masks import make_identity

F32 = mybir.dt.float32
BF16 = mybir.dt.bfloat16
U32 = mybir.dt.uint32
U8 = mybir.dt.uint8
FP8X4 = mybir.dt.float8_e4m3fn_x4
ACT = mybir.ActivationFunctionType
ALU = mybir.AluOpType

P = 128
PACK = 4
B = 64
BLOCKS = 2
DPB = 512
GATES = 3
R_GATE, C_GATE, Z_GATE = 0, 1, 2
CHUNKS = DPB // P
PAIRS = CHUNKS // 2
EPS = 1e-4

WHOLE = (0, DPB)
FIRST_HALF = (0, DPB // 2)
SECOND_HALF = (DPB // 2, DPB)

L1_VECTOR_SHARE = 11
L2_VECTOR_SHARE = 8

FLOPS = 2 * B * BLOCKS * (DPB * DPB + DPB * GATES * DPB)

HB_COL = 0
HG_COL = BLOCKS * CHUNKS
GB_COL = 2 * BLOCKS * CHUNKS
VEC_COLS = GB_COL + BLOCKS * GATES * CHUNKS


def tile_deter_pb_s_kernel(tc, hid0, deter, hw1, hb1, hg1, gw, gb, out):
    nc = tc.nc
    with tc.tile_pool(name="keep", bufs=1) as keep, tc.psum_pool(name="psum", bufs=1) as psum, tc.manual_schedule():
        layer1_keys = [("w1", j) for j in range(BLOCKS)]
        layer2_keys = [(g, j) for j in range(BLOCKS) for g in range(GATES)]
        raw, grouped, codes, scales = {}, {}, {}, {}
        for key in layer1_keys + layer2_keys:
            label = "%s_%d" % key
            raw[key] = keep.tile([P, PACK, DPB], BF16, name="raw_" + label)
            grouped[key] = keep.tile([P, DPB, PACK], BF16, name="grouped_" + label, align_bytes=64)
            codes[key] = keep.tile([P, DPB], U32, name="codes_" + label, align_bytes=64)
            scales[key] = keep.tile([P, DPB], U8, name="scales_" + label, align_bytes=64)

        def load_weights(key, cols):
            lo, hi = cols
            if key[0] == "w1":
                rows = hw1[key[1], :, lo:hi].rearrange("(p t) n -> p t n", t=PACK)
            else:
                g, j = key
                rows = gw[j, :, g * DPB + lo : g * DPB + hi].rearrange("(t p) n -> p t n", p=P)
            nc.sync.dma_start(out=raw[key][:, :, lo:hi], in_=rows)

        def split(key, cols):
            lo, hi = cols
            share = L1_VECTOR_SHARE if key[0] == "w1" else L2_VECTOR_SHARE
            return lo, lo + (hi - lo) * share // 16, hi

        def regroup_on_vector(key, cols):
            lo, mid, hi = split(key, cols)
            nc.vector.tensor_copy(
                out=grouped[key][:, lo:mid, :].rearrange("p (c i) t -> p c t i", i=4),
                in_=raw[key][:, :, lo:mid].rearrange("p t (c i) -> p c t i", i=4),
            )

        def regroup_on_scalar(key, cols):
            lo, mid, hi = split(key, cols)
            nc.scalar.copy(
                out=grouped[key][:, mid:hi, :].rearrange("p (c i) t -> p c t i", i=4),
                in_=raw[key][:, :, mid:hi].rearrange("p t (c i) -> p c t i", i=4),
            )

        def regroup(key, cols):
            regroup_on_vector(key, cols)
            regroup_on_scalar(key, cols)

        def quantise(key, cols):
            lo, hi = cols
            nc.vector.quantize_mx(
                out=codes[key][:, lo:hi].bitcast(FP8X4),
                scales=scales[key][:, lo:hi],
                in_=grouped[key][:, lo:hi, :].rearrange("p w t -> p (w t)"),
            )

        def multiply(key, cols, acc, moving_codes, moving_scales):
            j = key[1]
            for m in range(cols[0] // P, cols[1] // P):
                nc.tensor.matmul_mx(
                    out=acc[:, m, :],
                    lhsT=codes[key][:, m * P : (m + 1) * P].bitcast(FP8X4),
                    lhsT_scale=scales[key][:, m * P : (m + 1) * P],
                    rhs=moving_codes[:, j * B : (j + 1) * B].bitcast(FP8X4),
                    rhs_scale=moving_scales[:, j * B : (j + 1) * B],
                    start=True,
                    stop=True,
                )

        def spot(m):
            return m % PAIRS * 2 + m // PAIRS

        ident_f32 = keep.tile([P, P], F32, name="ident_f32")
        make_identity(nc, ident_f32[:])
        ident_bf = keep.tile([P, P], BF16, name="ident_bf")
        make_identity(nc, ident_bf[:])
        vec_rows = keep.tile([P, P], BF16, name="vec_rows")
        nc.vector.memset(vec_rows[:], 0.0)
        one_col = keep.tile([P, 1], F32, name="one_col")
        nc.vector.memset(one_col[:], 1.0)
        warm_col = keep.tile([P, 2], F32, name="warm_col")
        nc.scalar.activation(out=warm_col[:, 0:1], in_=one_col[:], func=ACT.Abs_reciprocal_sqrt)
        mean_w = keep.tile([P, P], F32, name="mean_w")
        nc.vector.memset(mean_w[:], 1.0 / (BLOCKS * DPB))
        eps_col = keep.tile([P, 1], F32, name="eps_col")
        nc.vector.memset(eps_col[:], EPS)

        x_sb = keep.tile([P, DPB], BF16, name="x_sb")
        d_sb = keep.tile([P, DPB], BF16, name="d_sb")
        out_view = out.rearrange("b (j h q f) -> h b j q f", j=BLOCKS, h=2, f=P)
        load_weights(("w1", 0), WHOLE)
        nc.sync.dma_start(out=x_sb[:], in_=hid0.rearrange("b (j k) -> (b j) k", j=BLOCKS))
        load_weights(("w1", 1), WHOLE)
        nc.sync.dma_start(out=vec_rows[HB_COL:HG_COL, :], in_=hb1.rearrange("(r p) -> r p", p=P))
        nc.sync.dma_start(out=vec_rows[HG_COL:GB_COL, :], in_=hg1.rearrange("(r p) -> r p", p=P))
        gb_rows = gb.rearrange("(r p) -> r p", p=P)
        nc.sync.dma_start(out=vec_rows[GB_COL : GB_COL + 16, :], in_=gb_rows[0:16, :])
        nc.sync.dma_start(out=vec_rows[GB_COL + 16 : VEC_COLS, :], in_=gb_rows[16 : VEC_COLS - GB_COL, :])
        load_weights((R_GATE, 0), WHOLE)
        load_weights((C_GATE, 0), WHOLE)
        nc.sync.dma_start(out=d_sb[:], in_=deter.rearrange("b (j k) -> (b j) k", j=BLOCKS))
        load_weights((Z_GATE, 0), WHOLE)
        load_weights((R_GATE, 1), WHOLE)
        load_weights((C_GATE, 1), WHOLE)
        load_weights((Z_GATE, 1), FIRST_HALF)
        load_weights((Z_GATE, 1), SECOND_HALF)

        xT_ps = psum.tile([P, 2, P], F32, name="xT_ps", tag="bank_0")
        vecT_ps = psum.tile([P, P], BF16, name="vecT_ps", tag="bank_1")
        dT_ps = psum.tile([P, CHUNKS, P], BF16, name="dT_ps", tag="bank_2")
        u_ps = [psum.tile([P, CHUNKS, B], F32, name="u_ps_%d" % j, tag="bank_%d" % (3 + j)) for j in range(BLOCKS)]

        x_words = x_sb[:].bitcast(F32).rearrange("p (w u) -> p u w", u=2)
        for u in range(2):
            nc.tensor.transpose(xT_ps[:, u, :], x_words[:, u, :], ident_f32[:])
        regroup(("w1", 0), WHOLE)
        x_grouped = keep.tile([P, P * PACK], BF16, name="x_grouped", align_bytes=64)
        nc.scalar.copy(
            out=x_grouped[:].bitcast(F32).rearrange("p (j b u) -> p j b u", j=BLOCKS, u=2),
            in_=xT_ps[:].rearrange("p u (b j) -> p j b u", j=BLOCKS),
        )
        x_codes = keep.tile([P, P], U32, name="x_codes", align_bytes=64)
        x_scales = keep.tile([P, P], U8, name="x_scales", align_bytes=64)
        quantise(("w1", 0), WHOLE)
        regroup(("w1", 1), WHOLE)
        nc.vector.quantize_mx(out=x_codes[:].bitcast(FP8X4), scales=x_scales[:], in_=x_grouped[:])
        quantise(("w1", 1), WHOLE)
        nc.tensor.transpose(vecT_ps[:], vec_rows[:], ident_bf[:])
        vec = keep.tile([P, VEC_COLS], F32, name="vec")
        nc.scalar.copy(out=vec[:], in_=vecT_ps[:, 0:VEC_COLS])

        def vec_col(first, c):
            return vec[:, first + c : first + c + 1]

        sq = keep.tile([P, BLOCKS, CHUNKS, B], F32, name="sq")
        sq_sum = keep.tile([P, BLOCKS, B], F32, name="sq_sum")
        gained = keep.tile([P, BLOCKS, CHUNKS, B], F32, name="gained")
        normed = keep.tile([P, BLOCKS, B, PACK], F32, name="normed")
        gate_h = keep.tile([P, BLOCKS, B, PACK], F32, name="gate_h")
        h_grouped = keep.tile([P, BLOCKS, B, PACK], BF16, name="h_grouped", align_bytes=64)
        h_codes = keep.tile([P, P], U32, name="h_codes", align_bytes=64)
        h_scales = keep.tile([P, P], U8, name="h_scales", align_bytes=64)
        mean_ps = psum.tile([P, B], F32, name="mean_ps", tag="bank_0")
        rstd = keep.tile([P, B], F32, name="rstd")

        def squares(j):
            for m in range(CHUNKS):
                nc.scalar.activation(
                    out=sq[:, j, m, :], in_=u_ps[j][:, m, :], func=ACT.Square,
                    bias=vec_col(HB_COL, j * CHUNKS + m), scale=1.0,
                )

        def mean_of_squares(j):
            nc.vector.tensor_reduce(
                out=sq_sum[:, j, :], in_=sq[:, j].rearrange("p m b -> p b m"), op=ALU.add, axis=mybir.AxisListType.X
            )
            nc.tensor.matmul(
                out=mean_ps[:], lhsT=mean_w[:], rhs=sq_sum[:, j, :], start=(j == 0), stop=(j == BLOCKS - 1)
            )

        def bias_and_gain(j):
            for m in range(CHUNKS):
                c = j * CHUNKS + m
                nc.vector.tensor_scalar(
                    out=gained[:, j, m, :], in0=u_ps[j][:, m, :],
                    scalar1=vec_col(HB_COL, c), scalar2=vec_col(HG_COL, c), op0=ALU.add, op1=ALU.mult,
                )

        def normalise(j):
            nc.vector.tensor_tensor(
                out=normed[:, j], in0=gained[:, j].rearrange("p t b -> p b t"),
                in1=rstd[:].unsqueeze(2).to_broadcast([P, B, PACK]), op=ALU.mult,
            )

        def silu_gate(j):
            nc.scalar.activation(
                out=gate_h[:, j].rearrange("p b t -> p (b t)"), in_=normed[:, j].rearrange("p b t -> p (b t)"),
                func=ACT.Sigmoid,
            )

        def silu_product(j):
            nc.vector.tensor_tensor(out=h_grouped[:, j], in0=normed[:, j], in1=gate_h[:, j], op=ALU.mult)

        multiply(("w1", 0), WHOLE, u_ps[0], x_codes, x_scales)
        multiply(("w1", 1), WHOLE, u_ps[1], x_codes, x_scales)
        regroup((R_GATE, 0), WHOLE)
        z_bias = vec[:, GB_COL:VEC_COLS].rearrange("p (j g m) -> p j g m", j=BLOCKS, g=GATES)[:, :, Z_GATE, :]
        nc.vector.tensor_scalar(out=z_bias, in0=z_bias, scalar1=-1.0, scalar2=1.0, op0=ALU.mult, op1=ALU.add)
        regroup_on_vector((C_GATE, 0), WHOLE)
        squares(0)
        mean_of_squares(0)
        quantise((R_GATE, 0), WHOLE)
        squares(1)
        mean_of_squares(1)
        regroup_on_scalar((C_GATE, 0), WHOLE)
        regroup((Z_GATE, 0), WHOLE)
        bias_and_gain(0)
        bias_and_gain(1)
        quantise((C_GATE, 0), WHOLE)
        nc.scalar.activation(out=rstd[:], in_=mean_ps[:], func=ACT.Abs_reciprocal_sqrt, bias=eps_col[:], scale=1.0)
        nc.scalar.activation(out=warm_col[:, 1:2], in_=one_col[:], func=ACT.Sigmoid)
        for j in range(BLOCKS):
            normalise(j)
            silu_gate(j)
        quantise((Z_GATE, 0), WHOLE)
        regroup((R_GATE, 1), WHOLE)
        for j in range(BLOCKS):
            silu_product(j)
        for j in range(BLOCKS):
            nc.vector.quantize_mx(
                out=h_codes[:, j * B : (j + 1) * B].bitcast(FP8X4),
                scales=h_scales[:, j * B : (j + 1) * B],
                in_=h_grouped[:, j].rearrange("p b t -> p (b t)"),
            )

        for m in range(CHUNKS):
            nc.tensor.transpose(dT_ps[:, spot(m), :], d_sb[:, m * P : (m + 1) * P], ident_bf[:])
        d_feat = dT_ps[:].rearrange("p m (b j) -> p j m b", j=BLOCKS)

        gate_ps = {}
        for j in range(BLOCKS):
            gate_ps[(R_GATE, j)] = psum.tile([P, CHUNKS, B], F32, name="r_ps_%d" % j, tag="bank_%d" % (3 + j))
        gate_ps[(C_GATE, 0)] = psum.tile([P, CHUNKS, B], F32, name="c_ps_0", tag="bank_1")
        gate_ps[(C_GATE, 1)] = psum.tile([P, CHUNKS, B], F32, name="c_ps_1", tag="bank_5")
        gate_ps[(Z_GATE, 0)] = psum.tile([P, CHUNKS, B], F32, name="z_ps_0", tag="bank_6")

        spare_ps = psum.tile([P, DPB], F32, name="spare_ps", tag="bank_7")
        reset = keep.tile([P, BLOCKS, CHUNKS, B], F32, name="reset")
        rc = keep.tile([P, BLOCKS, CHUNKS, B], F32, name="rc")
        minus_cand = keep.tile([P, BLOCKS, CHUNKS, B], F32, name="minus_cand")
        stay = keep.tile([P, BLOCKS, CHUNKS, B], F32, name="stay")
        old = keep.tile([P, BLOCKS, CHUNKS, B], F32, name="old")
        new = keep.tile([P, BLOCKS, CHUNKS, B], F32, name="new")
        result = keep.tile([P, BLOCKS, PAIRS, P], F32, name="result")
        sum_ps = {}

        def keep_clock(key):
            nc.tensor.matmul_mx(
                out=spare_ps[:],
                lhsT=codes[key][:, 0:P].bitcast(FP8X4),
                lhsT_scale=scales[key][:, 0:P],
                rhs=codes[key][:].bitcast(FP8X4),
                rhs_scale=scales[key][:],
                start=True,
                stop=True,
            )

        def gate_product(key, cols):
            multiply(key, cols, gate_ps[key], h_codes, h_scales)

        def sigmoid_gate(key, cols, dest, scale):
            g, j = key
            for m in range(cols[0] // P, cols[1] // P):
                nc.scalar.activation(
                    out=dest[:, j, spot(m), :], in_=gate_ps[key][:, m, :], func=ACT.Sigmoid,
                    bias=vec_col(GB_COL, (j * GATES + g) * CHUNKS + m), scale=scale,
                )

        def reset_gate(j):
            sigmoid_gate((R_GATE, j), WHOLE, reset, 1.0)

        def keep_gate(j, cols):
            sigmoid_gate((Z_GATE, j), cols, stay, -1.0)

        def reset_candidate(j):
            for m in range(CHUNKS):
                nc.vector.scalar_tensor_tensor(
                    out=rc[:, j, spot(m), :], in0=gate_ps[(C_GATE, j)][:, m, :],
                    scalar=vec_col(GB_COL, (j * GATES + C_GATE) * CHUNKS + m),
                    in1=reset[:, j, spot(m), :], op0=ALU.add, op1=ALU.mult,
                )

        def candidate(j):
            nc.scalar.activation(
                out=minus_cand[:, j].rearrange("p m b -> p (m b)"), in_=rc[:, j].rearrange("p m b -> p (m b)"),
                func=ACT.Tanh, scale=-1.0,
            )

        def old_part(j, lo, hi):
            nc.vector.tensor_tensor(out=old[:, j, lo:hi, :], in0=stay[:, j, lo:hi, :], in1=d_feat[:, j, lo:hi, :], op=ALU.mult)

        def new_part(j, lo, hi):
            nc.vector.scalar_tensor_tensor(
                out=new[:, j, lo:hi, :], in0=stay[:, j, lo:hi, :], scalar=1.0, in1=minus_cand[:, j, lo:hi, :],
                op0=ALU.subtract, op1=ALU.mult,
            )

        def to_tokens(part, j, q, first):
            if first:
                bank = 3 + j if q == 0 else j
                sum_ps[(j, q)] = psum.tile([P, P], F32, name="sum_ps_%d_%d" % (j, q), tag="bank_%d" % bank)
            nc.tensor.matmul(
                out=sum_ps[(j, q)][:], lhsT=part[:, j, 2 * q : 2 * q + 2, :].rearrange("p m b -> p (m b)"),
                rhs=ident_f32[:], start=first, stop=not first, is_transpose=True,
            )

        def new_state_on_scalar(j, q):
            nc.scalar.copy(out=result[:, j, q, :], in_=sum_ps[(j, q)][:])

        def new_state_on_vector(j, q):
            nc.vector.tensor_copy(out=result[:, j, q, :], in_=sum_ps[(j, q)][:])

        def store(j, engines):
            for h, engine in enumerate(engines):
                engine.dma_start(
                    out=out_view[h][:, j], in_=result[h * B : (h + 1) * B, j, :, :]
                )

        regroup((C_GATE, 1), WHOLE)
        quantise((R_GATE, 1), WHOLE)
        for key in ((C_GATE, 0), (C_GATE, 0), (Z_GATE, 0), (Z_GATE, 0)):
            keep_clock(key)
        for key in ((R_GATE, 0), (C_GATE, 0), (R_GATE, 1)):
            gate_product(key, WHOLE)
        gate_product((Z_GATE, 0), WHOLE)
        regroup((Z_GATE, 1), FIRST_HALF)
        quantise((C_GATE, 1), WHOLE)
        gate_product((C_GATE, 1), WHOLE)
        regroup((Z_GATE, 1), SECOND_HALF)
        quantise((Z_GATE, 1), FIRST_HALF)
        gate_ps[(Z_GATE, 1)] = psum.tile([P, CHUNKS, B], F32, name="z_ps_1", tag="bank_7")
        gate_product((Z_GATE, 1), FIRST_HALF)
        quantise((Z_GATE, 1), SECOND_HALF)
        gate_product((Z_GATE, 1), SECOND_HALF)
        reset_gate(0)
        reset_candidate(0)
        reset_gate(1)
        reset_candidate(1)
        keep_gate(0, WHOLE)
        candidate(0)
        keep_gate(1, FIRST_HALF)
        keep_gate(1, SECOND_HALF)
        candidate(1)
        old_part(0, 0, CHUNKS)
        new_part(0, 0, CHUNKS)
        for q in range(PAIRS):
            to_tokens(old, 0, q, True)
        for q in range(PAIRS):
            to_tokens(new, 0, q, False)
        old_part(1, 0, CHUNKS)
        for q in range(PAIRS):
            to_tokens(old, 1, q, True)
        for q in range(PAIRS):
            new_part(1, 2 * q, 2 * q + 2)
            to_tokens(new, 1, q, False)
        for q in range(PAIRS):
            new_state_on_scalar(0, q)
        store(0, (nc.sync, nc.sync))
        new_state_on_scalar(1, 0)
        new_state_on_vector(1, 1)
        store(1, (nc.sync, nc.scalar))
